import numpy as np
import ml_dtypes


def mxq(x, axis, fmt="e4m3"):
    dtype, down = {"e4m3": (ml_dtypes.float8_e4m3fn, 7), "e5m2": (ml_dtypes.float8_e5m2, 14)}[fmt]
    v = np.moveaxis(np.asarray(x, np.float32).astype(ml_dtypes.bfloat16).astype(np.float64), axis, -1)
    blocks = v.reshape(v.shape[:-1] + (-1, 32))
    amax = np.abs(blocks).max(-1, keepdims=True)
    byte = np.maximum(np.where(amax > 0, np.frexp(amax)[1] - 1 + 127, 0) - down, 1)
    scale = np.exp2(byte - 127.0)
    codes = (blocks / scale).astype(np.float32).astype(dtype).astype(np.float64)
    return np.moveaxis((codes * scale).reshape(v.shape), -1, axis)


WIDE = False


def mx_kscale(k):
    if not WIDE:
        return np.ones(k)
    levels = np.array([10, -10, 5, -5, 0])
    if k % 512:
        return np.exp2(np.random.permutation(np.resize(levels, k // 32))).repeat(32)
    a = np.empty((k // 512, 16))
    for p in range(k // 512):
        a[p, :8] = np.random.permutation(np.resize(levels, 8))
        for g in range(8):
            far = levels[np.abs(levels - a[p, g]) >= 10]
            a[p, g + 8] = far[np.random.randint(len(far))]
    return np.exp2(a.ravel()).repeat(32)


BF16 = ml_dtypes.bfloat16


def bf(x):
    return np.asarray(x, np.float32).astype(BF16)


def f64(x):
    return np.asarray(x).astype(np.float64)


B, H, W, S2, CIN, QDIM, KDIM, NH = 8, 32, 64, 2048, 1024, 64, 512, 1
HD = QDIM // NH
EPS = 1e-6


def layernorm(t, g, b):
    mu = t.mean(-1, keepdims=True)
    var = ((t - mu) ** 2).mean(-1, keepdims=True)
    return (t - mu) * (1.0 / np.sqrt(var + EPS)) * g + b


def setup_inputs():
    s = mx_kscale(KDIM)
    return {"y": bf(np.random.standard_normal((B, S2, KDIM)) * s),
            "wkv": bf(np.random.standard_normal((2 * QDIM, KDIM)) / np.sqrt(KDIM) / s[None, :]),
            "bkv": bf(np.random.standard_normal(2 * QDIM) * 0.3),
            "kn_g": bf(1.0 + 0.1 * np.random.standard_normal(HD)),
            "kn_b": bf(0.1 * np.random.standard_normal(HD))}


def reference(y, wkv, bkv, kn_g, kn_b):
    kv = (mxq(f64(y), 2, "e4m3") @ mxq(f64(wkv), 1, "e4m3").T) + f64(bkv)
    kv = kv.reshape(B, S2, 2, NH, HD).transpose(0, 2, 3, 1, 4)
    k, v = kv[:, 0], kv[:, 1]
    return layernorm(k, f64(kn_g), f64(kn_b)), v

@@ -1,0 +1,264 @@
+from contextlib import ExitStack
+
+import concourse.mybir as mybir
+from concourse.masks import make_identity
+
+F32 = mybir.dt.float32
+BF16 = mybir.dt.bfloat16
+U32 = mybir.dt.uint32
+U8 = mybir.dt.uint8
+FP8X4 = mybir.dt.float8_e4m3fn_x4
+ALU = mybir.AluOpType
+ACT = mybir.ActivationFunctionType
+
+P = 128
+K = 512
+ROW_WORDS = K // 2
+KEYS = 64
+ROWS = 8 * 2048
+EPS = 1e-6
+
+UNIT_TILES = 4
+UNIT_ROWS = UNIT_TILES * P
+BANK_TILES = 2
+BANK_ROWS = BANK_TILES * P
+UNIT_BANKS = UNIT_TILES // BANK_TILES
+CHUNK_TILES = 8
+CHUNK_UNITS = CHUNK_TILES // UNIT_TILES
+N_CHUNKS = ROWS // (CHUNK_TILES * P)
+N_UNITS = N_CHUNKS * CHUNK_UNITS
+
+VECTOR_EVERY = 8
+
+LAG_QUANTISE = 1
+LAG_PROJECT = 3
+LAG_BACK = 5
+LAG_CENTRE = 6
+LAG_DEVIATION = 9
+LAG_SCALE = 10
+N_STEPS = N_UNITS + LAG_SCALE
+
+FLOPS = 2 * ROWS * K * P
+
+
+def tile_crossattention2d_rope_pb_t_kernel(tc, y, wkv, bkv, kn_g, kn_b, out_0, out_1):
+    nc = tc.nc
+
+    y_chunks = y.flatten_outer_dims().rearrange("(c p j) k -> c p (j k)", p=P, j=CHUNK_TILES)
+    key_chunks = out_0.flatten_outer_dims().rearrange("(c p j) f -> c p (j f)", p=P, j=CHUNK_TILES)
+    value_chunks = out_1.flatten_outer_dims().rearrange("(c p j) f -> c p (j f)", p=P, j=CHUNK_TILES)
+
+    with ExitStack() as ctx:
+        ctx.enter_context(tc.manual_schedule())
+        consts = ctx.enter_context(tc.tile_pool(name="consts", bufs=1))
+        y_pool = ctx.enter_context(tc.tile_pool(name="y_pool", bufs=1))
+        grouped_pool = ctx.enter_context(tc.tile_pool(name="grouped_pool", bufs=4))
+        codes_pool = ctx.enter_context(tc.tile_pool(name="codes_pool", bufs=4))
+        xt_pool = ctx.enter_context(tc.tile_pool(name="xt_pool", bufs=4))
+        stats_pool = ctx.enter_context(tc.tile_pool(name="stats_pool", bufs=3))
+        chunk_pool = ctx.enter_context(tc.tile_pool(name="chunk_pool", bufs=4))
+        out_pool = ctx.enter_context(tc.tile_pool(name="out_pool", bufs=8))
+        words_psum = ctx.enter_context(tc.psum_pool(name="words_psum", bufs=3))
+        product_psum = ctx.enter_context(tc.psum_pool(name="product_psum", bufs=2))
+        rows_psum = ctx.enter_context(tc.psum_pool(name="rows_psum", bufs=3))
+
+        bias_bf16 = consts.tile([P, 1], BF16, name="bias_bf16")
+        gain_shift_bf16 = consts.tile([P, 2 * KEYS], BF16, name="gain_shift_bf16")
+        with nc.allow_non_contiguous_dma(reason="128 bias values, one to a partition"):
+            nc.sync.dma_start(out=bias_bf16[:], in_=bkv.rearrange("(f o) -> f o", o=1))
+        nc.sync.dma_start(out=gain_shift_bf16[:, 0:KEYS], in_=kn_g.partition_broadcast(P))
+        nc.sync.dma_start(out=gain_shift_bf16[:, KEYS : 2 * KEYS], in_=kn_b.partition_broadcast(P))
+        w_rows = consts.tile([P, K], BF16, name="w_rows")
+        nc.sync.dma_start(out=w_rows[:], in_=wkv)
+        y_rows = {}
+        for c in range(N_CHUNKS):
+            y_rows[c] = y_pool.tile([P, CHUNK_TILES * K], BF16, name="y_chunk_%d" % c)
+            nc.sync.dma_start(out=y_rows[c][:], in_=y_chunks[c])
+
+        eps = consts.tile([P, 1], F32, name="eps")
+        nc.vector.memset(eps[:], EPS)
+        table_warmer = consts.tile([P, 1], F32, name="table_warmer")
+        nc.scalar.activation(out=table_warmer[:], in_=eps[:], func=ACT.Sqrt)
+        identity = consts.tile([P, P], F32, name="identity")
+        make_identity(nc, identity[:])
+
+        w_words = words_psum.tile([P, 2, P], F32, tag="words", name="w_words")
+        for h in range(2):
+            nc.tensor.transpose(
+                w_words[:, h, :], w_rows[:].bitcast(F32)[:, h : ROW_WORDS : 2], identity[:]
+            )
+        w_grouped = consts.tile([P, 4 * P], BF16, name="w_grouped", align_bytes=64)
+        nc.vector.tensor_copy(
+            out=w_grouped[:].bitcast(F32).rearrange("p (f h) -> p f h", h=2),
+            in_=w_words[:].rearrange("p h f -> p f h"),
+        )
+        w_codes = consts.tile([P, P], U32, name="w_codes", align_bytes=64)
+        w_scales = consts.tile([P, P], U8, name="w_scales", align_bytes=64)
+        nc.vector.quantize_mx(out=w_codes[:].bitcast(FP8X4), scales=w_scales[:], in_=w_grouped[:])
+
+        bias = consts.tile([P, 1], F32, name="bias")
+        nc.vector.tensor_copy(out=bias[:], in_=bias_bf16[:])
+        gain_shift = consts.tile([P, 2 * KEYS], F32, name="gain_shift")
+        nc.vector.tensor_copy(out=gain_shift[:], in_=gain_shift_bf16[:])
+        gain = gain_shift[:, 0:KEYS]
+        shift = gain_shift[:, KEYS : 2 * KEYS]
+
+        grouped = {}
+        y_codes = {}
+        y_scales = {}
+        x_cols = {}
+        x_rows = {}
+        moments = {}
+        centred = {}
+        deviation = {}
+        rstd = {}
+        values = {}
+        keys = {}
+
+        def transpose_and_regroup(u):
+            words = y_rows[u // CHUNK_UNITS][:].bitcast(F32)
+            first_tile = (u % CHUNK_UNITS) * UNIT_TILES
+            grouped[u] = grouped_pool.tile([P, 4 * UNIT_ROWS], BF16, name="grouped", align_bytes=64)
+            pairs = grouped[u][:].bitcast(F32).rearrange("p (r h) -> p r h", h=2)
+            for b in range(UNIT_BANKS):
+                bank = words_psum.tile([P, 2, BANK_ROWS], F32, tag="words", name="bank")
+                for i in range(BANK_TILES):
+                    start = (first_tile + b * BANK_TILES + i) * ROW_WORDS
+                    for h in range(2):
+                        nc.tensor.transpose(
+                            bank[:, h, i * P : (i + 1) * P],
+                            words[:, start + h : start + ROW_WORDS : 2],
+                            identity[:],
+                        )
+                out = pairs[:, b * BANK_ROWS : (b + 1) * BANK_ROWS, :]
+                if (u * UNIT_BANKS + b) % VECTOR_EVERY == VECTOR_EVERY - 1:
+                    nc.vector.tensor_copy(out=out, in_=bank[:].rearrange("p h r -> p r h"))
+                else:
+                    nc.scalar.copy(out=out, in_=bank[:].rearrange("p h r -> p r h"))
+
+        def quantise(u):
+            y_codes[u] = codes_pool.tile([P, UNIT_ROWS], U32, name="y_codes", align_bytes=64)
+            y_scales[u] = codes_pool.tile([P, UNIT_ROWS], U8, name="y_scales", align_bytes=64)
+            nc.vector.quantize_mx(
+                out=y_codes[u][:].bitcast(FP8X4), scales=y_scales[u][:], in_=grouped[u][:]
+            )
+
+        def project_and_add_bias(u):
+            product = product_psum.tile([P, UNIT_ROWS], F32, name="product")
+            nc.tensor.matmul_mx(
+                out=product[:],
+                lhsT=w_codes[:].bitcast(FP8X4),
+                lhsT_scale=w_scales[:],
+                rhs=y_codes[u][:].bitcast(FP8X4),
+                rhs_scale=y_scales[u][:],
+                start=True,
+                stop=True,
+            )
+            x_cols[u] = xt_pool.tile([P, UNIT_ROWS], F32, name="x_cols")
+            nc.scalar.activation(
+                out=x_cols[u][:], in_=product[:], func=ACT.Identity, bias=bias[:, 0:1], scale=1.0
+            )
+
+        def transpose_back_and_take_values(u):
+            c = u // CHUNK_UNITS
+            first_tile = (u % CHUNK_UNITS) * UNIT_TILES
+            x_rows[u] = rows_psum.tile([P, UNIT_TILES, P], F32, tag="rows", name="x_rows")
+            for i in range(UNIT_TILES):
+                nc.tensor.transpose(x_rows[u][:, i, :], x_cols[u][:, i * P : (i + 1) * P], identity[:])
+            if first_tile == 0:
+                values[c] = out_pool.tile([P, CHUNK_TILES, KEYS], F32, name="values")
+            nc.scalar.copy(
+                out=values[c][:, first_tile : first_tile + UNIT_TILES, :], in_=x_rows[u][:, :, KEYS:P]
+            )
+            if first_tile + UNIT_TILES == CHUNK_TILES:
+                nc.sync.dma_start(out=value_chunks[c], in_=values[c][:].rearrange("p j f -> p (j f)"))
+
+        def mean_and_variance(u):
+            c = u // CHUNK_UNITS
+            first_tile = (u % CHUNK_UNITS) * UNIT_TILES
+            if first_tile == 0:
+                moments[c] = chunk_pool.tile([P, CHUNK_TILES, 2], F32, name="moments")
+            stats = stats_pool.tile([P, UNIT_TILES, 6], F32, name="stats")
+            for i in range(UNIT_TILES):
+                nc.vector.bn_stats(out=stats[:, i, :], in_=x_rows[u][:, i, 0:KEYS])
+            for i in range(UNIT_TILES):
+                nc.vector.bn_aggr(out=moments[c][:, first_tile + i, :], in_=stats[:, i, :])
+
+        def centre(u):
+            c = u // CHUNK_UNITS
+            first_tile = (u % CHUNK_UNITS) * UNIT_TILES
+            if first_tile == 0:
+                centred[c] = chunk_pool.tile([P, CHUNK_TILES, KEYS], F32, name="centred")
+            for i in range(UNIT_TILES):
+                nc.vector.scalar_tensor_tensor(
+                    out=centred[c][:, first_tile + i, :],
+                    in0=x_rows[u][:, i, 0:KEYS],
+                    scalar=moments[c][:, first_tile + i, 0:1],
+                    in1=gain,
+                    op0=ALU.subtract,
+                    op1=ALU.mult,
+                )
+
+        def standard_deviation(c):
+            deviation[c] = chunk_pool.tile([P, CHUNK_TILES, 1], F32, name="deviation")
+            nc.scalar.activation(
+                out=deviation[c][:], in_=moments[c][:, :, 1:2], func=ACT.Sqrt, bias=eps[:, 0:1], scale=1.0
+            )
+
+        def reciprocal(c):
+            rstd[c] = chunk_pool.tile([P, CHUNK_TILES, 1], F32, name="rstd")
+            nc.vector.reciprocal(out=rstd[c][:], in_=deviation[c][:])
+
+        def scale_shift_and_store(u):
+            c = u // CHUNK_UNITS
+            first_tile = (u % CHUNK_UNITS) * UNIT_TILES
+            if first_tile == 0:
+                keys[c] = out_pool.tile([P, CHUNK_TILES, KEYS], F32, name="keys")
+            for j in range(first_tile, first_tile + UNIT_TILES):
+                nc.vector.scalar_tensor_tensor(
+                    out=keys[c][:, j, :],
+                    in0=centred[c][:, j, :],
+                    scalar=rstd[c][:, j, :],
+                    in1=shift,
+                    op0=ALU.mult,
+                    op1=ALU.add,
+                )
+            if first_tile + UNIT_TILES == CHUNK_TILES:
+                nc.sync.dma_start(out=key_chunks[c], in_=keys[c][:].rearrange("p j f -> p (j f)"))
+
+        def unit_at(step, lag):
+            u = step - lag
+            return u if 0 <= u < N_UNITS else None
+
+        def chunk_at(step, lag):
+            u = step - lag
+            return u // CHUNK_UNITS if 0 <= u < N_UNITS and u % CHUNK_UNITS == 0 else None
+
+        for step in range(N_STEPS):
+            c = chunk_at(step, LAG_SCALE)
+            if c is not None:
+                reciprocal(c)
+            u = unit_at(step, LAG_BACK)
+            if u is not None:
+                transpose_back_and_take_values(u)
+            u = unit_at(step, LAG_CENTRE)
+            if u is not None:
+                mean_and_variance(u)
+            u = unit_at(step, 0)
+            if u is not None:
+                transpose_and_regroup(u)
+            u = unit_at(step, LAG_QUANTISE)
+            if u is not None:
+                quantise(u)
+            u = unit_at(step, LAG_CENTRE)
+            if u is not None:
+                centre(u)
+            u = unit_at(step, LAG_PROJECT)
+            if u is not None:
+                project_and_add_bias(u)
+            c = chunk_at(step, LAG_DEVIATION)
+            if c is not None:
+                standard_deviation(c)
+            u = unit_at(step, LAG_SCALE)
+            if u is not None:
+                scale_shift_and_store(u)

@@ -10,6 +10,7 @@ U8 = mybir.dt.uint8
 FP8X4 = mybir.dt.float8_e4m3fn_x4
 ALU = mybir.AluOpType
 ACT = mybir.ActivationFunctionType
+AXIS = mybir.AxisListType
 
 P = 128
 K = 512
@@ -28,15 +29,15 @@ CHUNK_UNITS = CHUNK_TILES // UNIT_TILES
 N_CHUNKS = ROWS // (CHUNK_TILES * P)
 N_UNITS = N_CHUNKS * CHUNK_UNITS
 
-VECTOR_EVERY = 8
-
 LAG_QUANTISE = 1
-LAG_PROJECT = 3
-LAG_BACK = 5
-LAG_CENTRE = 6
-LAG_DEVIATION = 9
-LAG_SCALE = 10
-N_STEPS = N_UNITS + LAG_SCALE
+LAG_PROJECT = 2
+LAG_BIAS = 3
+LAG_SUM = 4
+LAG_SQUARE = 5
+LAG_DEVIATION = 7
+LAG_NORMALISE = 8
+LAG_AFFINE = 9
+N_STEPS = N_UNITS + LAG_AFFINE
 
 FLOPS = 2 * ROWS * K * P
 
@@ -54,20 +55,18 @@ def tile_crossattention2d_rope_pb_t_kernel(tc, y, wkv, bkv, kn_g, kn_b, out_0, o
         y_pool = ctx.enter_context(tc.tile_pool(name="y_pool", bufs=1))
         grouped_pool = ctx.enter_context(tc.tile_pool(name="grouped_pool", bufs=4))
         codes_pool = ctx.enter_context(tc.tile_pool(name="codes_pool", bufs=4))
-        xt_pool = ctx.enter_context(tc.tile_pool(name="xt_pool", bufs=4))
-        stats_pool = ctx.enter_context(tc.tile_pool(name="stats_pool", bufs=3))
-        chunk_pool = ctx.enter_context(tc.tile_pool(name="chunk_pool", bufs=4))
-        out_pool = ctx.enter_context(tc.tile_pool(name="out_pool", bufs=8))
-        words_psum = ctx.enter_context(tc.psum_pool(name="words_psum", bufs=3))
-        product_psum = ctx.enter_context(tc.psum_pool(name="product_psum", bufs=2))
-        rows_psum = ctx.enter_context(tc.psum_pool(name="rows_psum", bufs=3))
+        x_pool = ctx.enter_context(tc.tile_pool(name="x_pool", bufs=6))
+        stat_pool = ctx.enter_context(tc.tile_pool(name="stat_pool", bufs=6))
+        junk_pool = ctx.enter_context(tc.tile_pool(name="junk_pool", bufs=2))
+        xhat_pool = ctx.enter_context(tc.tile_pool(name="xhat_pool", bufs=3))
+        out_pool = ctx.enter_context(tc.tile_pool(name="out_pool", bufs=4))
+        words_psum = ctx.enter_context(tc.psum_pool(name="words_psum", bufs=4))
+        product_psum = ctx.enter_context(tc.psum_pool(name="product_psum", bufs=4))
 
-        bias_bf16 = consts.tile([P, 1], BF16, name="bias_bf16")
-        gain_shift_bf16 = consts.tile([P, 2 * KEYS], BF16, name="gain_shift_bf16")
-        with nc.allow_non_contiguous_dma(reason="128 bias values, one to a partition"):
-            nc.sync.dma_start(out=bias_bf16[:], in_=bkv.rearrange("(f o) -> f o", o=1))
-        nc.sync.dma_start(out=gain_shift_bf16[:, 0:KEYS], in_=kn_g.partition_broadcast(P))
-        nc.sync.dma_start(out=gain_shift_bf16[:, KEYS : 2 * KEYS], in_=kn_b.partition_broadcast(P))
+        vectors_bf16 = consts.tile([P, 2 * P], BF16, name="vectors_bf16")
+        nc.sync.dma_start(out=vectors_bf16[:, 0:P], in_=bkv.partition_broadcast(P))
+        nc.sync.dma_start(out=vectors_bf16[:, P : P + KEYS], in_=kn_g.partition_broadcast(P))
+        nc.sync.dma_start(out=vectors_bf16[:, P + KEYS : 2 * P], in_=kn_b.partition_broadcast(P))
         w_rows = consts.tile([P, K], BF16, name="w_rows")
         nc.sync.dma_start(out=w_rows[:], in_=wkv)
         y_rows = {}
@@ -84,9 +83,7 @@ def tile_crossattention2d_rope_pb_t_kernel(tc, y, wkv, bkv, kn_g, kn_b, out_0, o
 
         w_words = words_psum.tile([P, 2, P], F32, tag="words", name="w_words")
         for h in range(2):
-            nc.tensor.transpose(
-                w_words[:, h, :], w_rows[:].bitcast(F32)[:, h : ROW_WORDS : 2], identity[:]
-            )
+            nc.tensor.transpose(w_words[:, h, :], w_rows[:].bitcast(F32)[:, h : ROW_WORDS : 2], identity[:])
         w_grouped = consts.tile([P, 4 * P], BF16, name="w_grouped", align_bytes=64)
         nc.vector.tensor_copy(
             out=w_grouped[:].bitcast(F32).rearrange("p (f h) -> p f h", h=2),
@@ -96,134 +93,158 @@ def tile_crossattention2d_rope_pb_t_kernel(tc, y, wkv, bkv, kn_g, kn_b, out_0, o
         w_scales = consts.tile([P, P], U8, name="w_scales", align_bytes=64)
         nc.vector.quantize_mx(out=w_codes[:].bitcast(FP8X4), scales=w_scales[:], in_=w_grouped[:])
 
-        bias = consts.tile([P, 1], F32, name="bias")
-        nc.vector.tensor_copy(out=bias[:], in_=bias_bf16[:])
-        gain_shift = consts.tile([P, 2 * KEYS], F32, name="gain_shift")
-        nc.vector.tensor_copy(out=gain_shift[:], in_=gain_shift_bf16[:])
-        gain = gain_shift[:, 0:KEYS]
-        shift = gain_shift[:, KEYS : 2 * KEYS]
+        bias = consts.tile([P, UNIT_TILES, P], F32, name="bias")
+        gain = consts.tile([P, UNIT_TILES, KEYS], F32, name="gain")
+        shift = consts.tile([P, UNIT_TILES, KEYS], F32, name="shift")
+        for i in range(UNIT_TILES):
+            nc.vector.tensor_copy(out=bias[:, i, :], in_=vectors_bf16[:, 0:P])
+            nc.vector.tensor_copy(out=gain[:, i, :], in_=vectors_bf16[:, P : P + KEYS])
+            nc.vector.tensor_copy(out=shift[:, i, :], in_=vectors_bf16[:, P + KEYS : 2 * P])
 
         grouped = {}
         y_codes = {}
         y_scales = {}
-        x_cols = {}
-        x_rows = {}
-        moments = {}
-        centred = {}
+        product = {}
+        x = {}
+        sums = {}
+        squares = {}
         deviation = {}
         rstd = {}
-        values = {}
+        offset = {}
+        xhat = {}
         keys = {}
 
+        def place(u):
+            return u // CHUNK_UNITS, (u % CHUNK_UNITS) * UNIT_TILES
+
         def transpose_and_regroup(u):
-            words = y_rows[u // CHUNK_UNITS][:].bitcast(F32)
-            first_tile = (u % CHUNK_UNITS) * UNIT_TILES
+            c, first = place(u)
+            words = y_rows[c][:].bitcast(F32)
             grouped[u] = grouped_pool.tile([P, 4 * UNIT_ROWS], BF16, name="grouped", align_bytes=64)
             pairs = grouped[u][:].bitcast(F32).rearrange("p (r h) -> p r h", h=2)
+            banks = []
             for b in range(UNIT_BANKS):
                 bank = words_psum.tile([P, 2, BANK_ROWS], F32, tag="words", name="bank")
+                banks.append(bank)
                 for i in range(BANK_TILES):
-                    start = (first_tile + b * BANK_TILES + i) * ROW_WORDS
+                    start = (first + b * BANK_TILES + i) * ROW_WORDS
                     for h in range(2):
                         nc.tensor.transpose(
-                            bank[:, h, i * P : (i + 1) * P],
-                            words[:, start + h : start + ROW_WORDS : 2],
-                            identity[:],
+                            bank[:, h, i * P : (i + 1) * P], words[:, start + h : start + ROW_WORDS : 2], identity[:]
                         )
-                out = pairs[:, b * BANK_ROWS : (b + 1) * BANK_ROWS, :]
-                if (u * UNIT_BANKS + b) % VECTOR_EVERY == VECTOR_EVERY - 1:
-                    nc.vector.tensor_copy(out=out, in_=bank[:].rearrange("p h r -> p r h"))
-                else:
-                    nc.scalar.copy(out=out, in_=bank[:].rearrange("p h r -> p r h"))
+            return pairs, banks
+
+        def regroup(pairs, banks, b):
+            nc.scalar.copy(
+                out=pairs[:, b * BANK_ROWS : (b + 1) * BANK_ROWS, :], in_=banks[b][:].rearrange("p h r -> p r h")
+            )
 
         def quantise(u):
             y_codes[u] = codes_pool.tile([P, UNIT_ROWS], U32, name="y_codes", align_bytes=64)
             y_scales[u] = codes_pool.tile([P, UNIT_ROWS], U8, name="y_scales", align_bytes=64)
-            nc.vector.quantize_mx(
-                out=y_codes[u][:].bitcast(FP8X4), scales=y_scales[u][:], in_=grouped[u][:]
+            nc.vector.quantize_mx(out=y_codes[u][:].bitcast(FP8X4), scales=y_scales[u][:], in_=grouped[u][:])
+
+        def project(u):
+            product[u] = product_psum.tile([P, UNIT_TILES, P], F32, name="product")
+            for i in range(UNIT_TILES):
+                nc.tensor.matmul_mx(
+                    out=product[u][:, i, :],
+                    lhsT=y_codes[u][:, i * P : (i + 1) * P].bitcast(FP8X4),
+                    lhsT_scale=y_scales[u][:, i * P : (i + 1) * P],
+                    rhs=w_codes[:].bitcast(FP8X4),
+                    rhs_scale=w_scales[:],
+                    start=True,
+                    stop=True,
+                )
+
+        def add_bias(u):
+            c, first = place(u)
+            if first == 0:
+                x[c] = x_pool.tile([P, 2, CHUNK_TILES, KEYS], F32, name="x")
+            nc.vector.tensor_tensor(
+                out=x[c][:, :, first : first + UNIT_TILES, :].rearrange("p h j f -> p j h f"),
+                in0=product[u][:].rearrange("p j (h f) -> p j h f", h=2),
+                in1=bias[:].rearrange("p j (h f) -> p j h f", h=2),
+                op=ALU.add,
+            )
+            if first + UNIT_TILES == CHUNK_TILES:
+                nc.sync.dma_start(out=value_chunks[c], in_=x[c][:, 1, :, :].rearrange("p j f -> p (j f)"))
+
+        def row_sums(u):
+            c, first = place(u)
+            if first == 0:
+                sums[c] = stat_pool.tile([P, CHUNK_TILES], F32, name="sums")
+            nc.vector.tensor_reduce(
+                out=sums[c][:, first : first + UNIT_TILES],
+                in_=x[c][:, 0, first : first + UNIT_TILES, :],
+                axis=AXIS.X,
+                op=ALU.add,
             )
 
-        def project_and_add_bias(u):
-            product = product_psum.tile([P, UNIT_ROWS], F32, name="product")
-            nc.tensor.matmul_mx(
-                out=product[:],
-                lhsT=w_codes[:].bitcast(FP8X4),
-                lhsT_scale=w_scales[:],
-                rhs=y_codes[u][:].bitcast(FP8X4),
-                rhs_scale=y_scales[u][:],
-                start=True,
-                stop=True,
-            )
-            x_cols[u] = xt_pool.tile([P, UNIT_ROWS], F32, name="x_cols")
-            nc.scalar.activation(
-                out=x_cols[u][:], in_=product[:], func=ACT.Identity, bias=bias[:, 0:1], scale=1.0
-            )
-
-        def transpose_back_and_take_values(u):
-            c = u // CHUNK_UNITS
-            first_tile = (u % CHUNK_UNITS) * UNIT_TILES
-            x_rows[u] = rows_psum.tile([P, UNIT_TILES, P], F32, tag="rows", name="x_rows")
-            for i in range(UNIT_TILES):
-                nc.tensor.transpose(x_rows[u][:, i, :], x_cols[u][:, i * P : (i + 1) * P], identity[:])
-            if first_tile == 0:
-                values[c] = out_pool.tile([P, CHUNK_TILES, KEYS], F32, name="values")
-            nc.scalar.copy(
-                out=values[c][:, first_tile : first_tile + UNIT_TILES, :], in_=x_rows[u][:, :, KEYS:P]
-            )
-            if first_tile + UNIT_TILES == CHUNK_TILES:
-                nc.sync.dma_start(out=value_chunks[c], in_=values[c][:].rearrange("p j f -> p (j f)"))
-
-        def mean_and_variance(u):
-            c = u // CHUNK_UNITS
-            first_tile = (u % CHUNK_UNITS) * UNIT_TILES
-            if first_tile == 0:
-                moments[c] = chunk_pool.tile([P, CHUNK_TILES, 2], F32, name="moments")
-            stats = stats_pool.tile([P, UNIT_TILES, 6], F32, name="stats")
-            for i in range(UNIT_TILES):
-                nc.vector.bn_stats(out=stats[:, i, :], in_=x_rows[u][:, i, 0:KEYS])
-            for i in range(UNIT_TILES):
-                nc.vector.bn_aggr(out=moments[c][:, first_tile + i, :], in_=stats[:, i, :])
-
-        def centre(u):
-            c = u // CHUNK_UNITS
-            first_tile = (u % CHUNK_UNITS) * UNIT_TILES
-            if first_tile == 0:
-                centred[c] = chunk_pool.tile([P, CHUNK_TILES, KEYS], F32, name="centred")
-            for i in range(UNIT_TILES):
-                nc.vector.scalar_tensor_tensor(
-                    out=centred[c][:, first_tile + i, :],
-                    in0=x_rows[u][:, i, 0:KEYS],
-                    scalar=moments[c][:, first_tile + i, 0:1],
-                    in1=gain,
-                    op0=ALU.subtract,
-                    op1=ALU.mult,
+        def squared_deviations(u):
+            c, first = place(u)
+            if first == 0:
+                squares[c] = stat_pool.tile([P, CHUNK_TILES], F32, name="squares")
+            for j in range(first, first + UNIT_TILES):
+                junk = junk_pool.tile([P, KEYS], F32, name="junk")
+                nc.scalar.activation(
+                    out=junk[:],
+                    in_=x[c][:, 0, j, :],
+                    func=ACT.Square,
+                    bias=sums[c][:, j : j + 1],
+                    scale=-float(KEYS),
+                    accum_out=squares[c][:, j : j + 1],
                 )
 
         def standard_deviation(c):
-            deviation[c] = chunk_pool.tile([P, CHUNK_TILES, 1], F32, name="deviation")
+            deviation[c] = stat_pool.tile([P, CHUNK_TILES], F32, name="deviation")
             nc.scalar.activation(
-                out=deviation[c][:], in_=moments[c][:, :, 1:2], func=ACT.Sqrt, bias=eps[:, 0:1], scale=1.0
+                out=deviation[c][:], in_=squares[c][:], func=ACT.Sqrt, bias=eps[:, 0:1], scale=1.0 / KEYS**3
             )
 
-        def reciprocal(c):
-            rstd[c] = chunk_pool.tile([P, CHUNK_TILES, 1], F32, name="rstd")
+        def row_factors(c):
+            rstd[c] = stat_pool.tile([P, CHUNK_TILES], F32, name="rstd")
             nc.vector.reciprocal(out=rstd[c][:], in_=deviation[c][:])
 
-        def scale_shift_and_store(u):
-            c = u // CHUNK_UNITS
-            first_tile = (u % CHUNK_UNITS) * UNIT_TILES
-            if first_tile == 0:
-                keys[c] = out_pool.tile([P, CHUNK_TILES, KEYS], F32, name="keys")
-            for j in range(first_tile, first_tile + UNIT_TILES):
-                nc.vector.scalar_tensor_tensor(
-                    out=keys[c][:, j, :],
-                    in0=centred[c][:, j, :],
-                    scalar=rstd[c][:, j, :],
-                    in1=shift,
-                    op0=ALU.mult,
-                    op1=ALU.add,
+        def row_offsets(c):
+            offset[c] = stat_pool.tile([P, CHUNK_TILES], F32, name="offset")
+            nc.vector.scalar_tensor_tensor(
+                out=offset[c][:], in0=sums[c][:], scalar=-1.0 / KEYS, in1=rstd[c][:], op0=ALU.mult, op1=ALU.mult
+            )
+
+        def normalise(u):
+            c, first = place(u)
+            if first == 0:
+                xhat[c] = xhat_pool.tile([P, CHUNK_TILES, KEYS], F32, name="xhat")
+            for j in range(first, first + UNIT_TILES):
+                nc.scalar.activation(
+                    out=xhat[c][:, j, :],
+                    in_=x[c][:, 0, j, :],
+                    func=ACT.Identity,
+                    bias=offset[c][:, j : j + 1],
+                    scale=rstd[c][:, j : j + 1],
                 )
-            if first_tile + UNIT_TILES == CHUNK_TILES:
+
+        def apply_gain(u):
+            c, first = place(u)
+            if first == 0:
+                keys[c] = out_pool.tile([P, CHUNK_TILES, KEYS], F32, name="keys")
+            nc.vector.tensor_tensor(
+                out=keys[c][:, first : first + UNIT_TILES, :],
+                in0=xhat[c][:, first : first + UNIT_TILES, :],
+                in1=gain[:],
+                op=ALU.mult,
+            )
+
+        def apply_shift(u):
+            c, first = place(u)
+            nc.vector.tensor_tensor(
+                out=keys[c][:, first : first + UNIT_TILES, :],
+                in0=keys[c][:, first : first + UNIT_TILES, :],
+                in1=shift[:],
+                op=ALU.add,
+            )
+            if first + UNIT_TILES == CHUNK_TILES:
                 nc.sync.dma_start(out=key_chunks[c], in_=keys[c][:].rearrange("p j f -> p (j f)"))
 
         def unit_at(step, lag):
@@ -235,30 +256,39 @@ def tile_crossattention2d_rope_pb_t_kernel(tc, y, wkv, bkv, kn_g, kn_b, out_0, o
             return u // CHUNK_UNITS if 0 <= u < N_UNITS and u % CHUNK_UNITS == 0 else None
 
         for step in range(N_STEPS):
-            c = chunk_at(step, LAG_SCALE)
-            if c is not None:
-                reciprocal(c)
-            u = unit_at(step, LAG_BACK)
+            c_dev = chunk_at(step, LAG_DEVIATION)
+            if c_dev is not None:
+                standard_deviation(c_dev)
+            u_new = unit_at(step, 0)
+            if u_new is not None:
+                pairs, banks = transpose_and_regroup(u_new)
+                regroup(pairs, banks, 0)
+            u = unit_at(step, LAG_PROJECT)
             if u is not None:
-                transpose_back_and_take_values(u)
-            u = unit_at(step, LAG_CENTRE)
+                project(u)
+            u_aff = unit_at(step, LAG_AFFINE)
+            if u_aff is not None:
+                apply_gain(u_aff)
+            u = unit_at(step, LAG_SUM)
             if u is not None:
-                mean_and_variance(u)
-            u = unit_at(step, 0)
+                row_sums(u)
+            u = unit_at(step, LAG_SQUARE)
             if u is not None:
-                transpose_and_regroup(u)
+                squared_deviations(u)
             u = unit_at(step, LAG_QUANTISE)
             if u is not None:
                 quantise(u)
-            u = unit_at(step, LAG_CENTRE)
+            if c_dev is not None:
+                row_factors(c_dev)
+            if u_new is not None:
+                regroup(pairs, banks, 1)
+            if u_aff is not None:
+                apply_shift(u_aff)
+            u = unit_at(step, LAG_BIAS)
             if u is not None:
-                centre(u)
-            u = unit_at(step, LAG_PROJECT)
+                add_bias(u)
+            if c_dev is not None:
+                row_offsets(c_dev)
+            u = unit_at(step, LAG_NORMALISE)
             if u is not None:
-                project_and_add_bias(u)
-            c = chunk_at(step, LAG_DEVIATION)
-            if c is not None:
-                standard_deviation(c)
-            u = unit_at(step, LAG_SCALE)
-            if u is not None:
-                scale_shift_and_store(u)
+                normalise(u)

@@ -32,12 +32,15 @@ N_UNITS = N_CHUNKS * CHUNK_UNITS
 LAG_QUANTISE = 1
 LAG_PROJECT = 2
 LAG_BIAS = 3
-LAG_SUM = 4
-LAG_SQUARE = 5
-LAG_DEVIATION = 7
-LAG_NORMALISE = 8
+LAG_MOMENTS = 4
+LAG_DEVIATION = 6
+LAG_NORMALISE = 7
 LAG_AFFINE = 9
 N_STEPS = N_UNITS + LAG_AFFINE
+
+LOADS_AHEAD = 6
+
+VECTOR_EVERY = 1000
 
 FLOPS = 2 * ROWS * K * P
 
@@ -57,22 +60,26 @@ def tile_crossattention2d_rope_pb_t_kernel(tc, y, wkv, bkv, kn_g, kn_b, out_0, o
         codes_pool = ctx.enter_context(tc.tile_pool(name="codes_pool", bufs=4))
         x_pool = ctx.enter_context(tc.tile_pool(name="x_pool", bufs=6))
         stat_pool = ctx.enter_context(tc.tile_pool(name="stat_pool", bufs=6))
-        junk_pool = ctx.enter_context(tc.tile_pool(name="junk_pool", bufs=2))
-        xhat_pool = ctx.enter_context(tc.tile_pool(name="xhat_pool", bufs=3))
+        xhat_pool = ctx.enter_context(tc.tile_pool(name="xhat_pool", bufs=4))
         out_pool = ctx.enter_context(tc.tile_pool(name="out_pool", bufs=4))
         words_psum = ctx.enter_context(tc.psum_pool(name="words_psum", bufs=4))
         product_psum = ctx.enter_context(tc.psum_pool(name="product_psum", bufs=4))
 
+        w_rows = consts.tile([P, K], BF16, name="w_rows")
+        nc.sync.dma_start(out=w_rows[:], in_=wkv)
         vectors_bf16 = consts.tile([P, 2 * P], BF16, name="vectors_bf16")
+        y_rows = {}
+
+        def load(c):
+            y_rows[c] = y_pool.tile([P, CHUNK_TILES * K], BF16, name="y_chunk_%d" % c)
+            nc.sync.dma_start(out=y_rows[c][:], in_=y_chunks[c])
+
+        load(0)
         nc.sync.dma_start(out=vectors_bf16[:, 0:P], in_=bkv.partition_broadcast(P))
         nc.sync.dma_start(out=vectors_bf16[:, P : P + KEYS], in_=kn_g.partition_broadcast(P))
         nc.sync.dma_start(out=vectors_bf16[:, P + KEYS : 2 * P], in_=kn_b.partition_broadcast(P))
-        w_rows = consts.tile([P, K], BF16, name="w_rows")
-        nc.sync.dma_start(out=w_rows[:], in_=wkv)
-        y_rows = {}
-        for c in range(N_CHUNKS):
-            y_rows[c] = y_pool.tile([P, CHUNK_TILES * K], BF16, name="y_chunk_%d" % c)
-            nc.sync.dma_start(out=y_rows[c][:], in_=y_chunks[c])
+        for c in range(1, LOADS_AHEAD):
+            load(c)
 
         eps = consts.tile([P, 1], F32, name="eps")
         nc.vector.memset(eps[:], EPS)
@@ -94,20 +101,22 @@ def tile_crossattention2d_rope_pb_t_kernel(tc, y, wkv, bkv, kn_g, kn_b, out_0, o
         nc.vector.quantize_mx(out=w_codes[:].bitcast(FP8X4), scales=w_scales[:], in_=w_grouped[:])
 
         bias = consts.tile([P, UNIT_TILES, P], F32, name="bias")
-        gain = consts.tile([P, UNIT_TILES, KEYS], F32, name="gain")
-        shift = consts.tile([P, UNIT_TILES, KEYS], F32, name="shift")
-        for i in range(UNIT_TILES):
-            nc.vector.tensor_copy(out=bias[:, i, :], in_=vectors_bf16[:, 0:P])
-            nc.vector.tensor_copy(out=gain[:, i, :], in_=vectors_bf16[:, P : P + KEYS])
-            nc.vector.tensor_copy(out=shift[:, i, :], in_=vectors_bf16[:, P + KEYS : 2 * P])
+        gain = consts.tile([P, CHUNK_TILES, KEYS], F32, name="gain")
+        shift = consts.tile([P, CHUNK_TILES, KEYS], F32, name="shift")
+
+        def spread_vectors():
+            for i in range(UNIT_TILES):
+                nc.vector.tensor_copy(out=bias[:, i, :], in_=vectors_bf16[:, 0:P])
+            for j in range(CHUNK_TILES):
+                nc.gpsimd.tensor_copy(out=gain[:, j, :], in_=vectors_bf16[:, P : P + KEYS])
+                nc.gpsimd.tensor_copy(out=shift[:, j, :], in_=vectors_bf16[:, P + KEYS : 2 * P])
 
         grouped = {}
         y_codes = {}
         y_scales = {}
         product = {}
         x = {}
-        sums = {}
-        squares = {}
+        moments = {}
         deviation = {}
         rstd = {}
         offset = {}
@@ -134,10 +143,9 @@ def tile_crossattention2d_rope_pb_t_kernel(tc, y, wkv, bkv, kn_g, kn_b, out_0, o
                         )
             return pairs, banks
 
-        def regroup(pairs, banks, b):
-            nc.scalar.copy(
-                out=pairs[:, b * BANK_ROWS : (b + 1) * BANK_ROWS, :], in_=banks[b][:].rearrange("p h r -> p r h")
-            )
+        def regroup(u, pairs, banks, b):
+            engine = nc.vector.tensor_copy if (u * UNIT_BANKS + b) % VECTOR_EVERY == VECTOR_EVERY - 1 else nc.scalar.copy
+            engine(out=pairs[:, b * BANK_ROWS : (b + 1) * BANK_ROWS, :], in_=banks[b][:].rearrange("p h r -> p r h"))
 
         def quantise(u):
             y_codes[u] = codes_pool.tile([P, UNIT_ROWS], U32, name="y_codes", align_bytes=64)
@@ -170,36 +178,20 @@ def tile_crossattention2d_rope_pb_t_kernel(tc, y, wkv, bkv, kn_g, kn_b, out_0, o
             if first + UNIT_TILES == CHUNK_TILES:
                 nc.sync.dma_start(out=value_chunks[c], in_=x[c][:, 1, :, :].rearrange("p j f -> p (j f)"))
 
-        def row_sums(u):
+        def moments_of_pairs(u):
             c, first = place(u)
             if first == 0:
-                sums[c] = stat_pool.tile([P, CHUNK_TILES], F32, name="sums")
-            nc.vector.tensor_reduce(
-                out=sums[c][:, first : first + UNIT_TILES],
-                in_=x[c][:, 0, first : first + UNIT_TILES, :],
-                axis=AXIS.X,
-                op=ALU.add,
-            )
-
-        def squared_deviations(u):
-            c, first = place(u)
-            if first == 0:
-                squares[c] = stat_pool.tile([P, CHUNK_TILES], F32, name="squares")
-            for j in range(first, first + UNIT_TILES):
-                junk = junk_pool.tile([P, KEYS], F32, name="junk")
-                nc.scalar.activation(
-                    out=junk[:],
-                    in_=x[c][:, 0, j, :],
-                    func=ACT.Square,
-                    bias=sums[c][:, j : j + 1],
-                    scale=-float(KEYS),
-                    accum_out=squares[c][:, j : j + 1],
+                moments[c] = stat_pool.tile([P, CHUNK_TILES, 3], F32, name="moments")
+            for j in range(first, first + UNIT_TILES, 2):
+                nc.vector.bn_stats(
+                    out=moments[c][:, j : j + 2, :].rearrange("p j m -> p (j m)"),
+                    in_=x[c][:, 0, j : j + 2, :].rearrange("p j f -> p f j"),
                 )
 
         def standard_deviation(c):
             deviation[c] = stat_pool.tile([P, CHUNK_TILES], F32, name="deviation")
             nc.scalar.activation(
-                out=deviation[c][:], in_=squares[c][:], func=ACT.Sqrt, bias=eps[:, 0:1], scale=1.0 / KEYS**3
+                out=deviation[c][:], in_=moments[c][:, :, 2], func=ACT.Sqrt, bias=eps[:, 0:1], scale=1.0 / KEYS
             )
 
         def row_factors(c):
@@ -209,14 +201,14 @@ def tile_crossattention2d_rope_pb_t_kernel(tc, y, wkv, bkv, kn_g, kn_b, out_0, o
         def row_offsets(c):
             offset[c] = stat_pool.tile([P, CHUNK_TILES], F32, name="offset")
             nc.vector.scalar_tensor_tensor(
-                out=offset[c][:], in0=sums[c][:], scalar=-1.0 / KEYS, in1=rstd[c][:], op0=ALU.mult, op1=ALU.mult
+                out=offset[c][:], in0=moments[c][:, :, 1], scalar=-1.0, in1=rstd[c][:], op0=ALU.mult, op1=ALU.mult
             )
 
-        def normalise(u):
+        def normalise(u, half):
             c, first = place(u)
-            if first == 0:
+            if first == 0 and half == 0:
                 xhat[c] = xhat_pool.tile([P, CHUNK_TILES, KEYS], F32, name="xhat")
-            for j in range(first, first + UNIT_TILES):
+            for j in range(first + 2 * half, first + 2 * half + 2):
                 nc.scalar.activation(
                     out=xhat[c][:, j, :],
                     in_=x[c][:, 0, j, :],
@@ -225,27 +217,11 @@ def tile_crossattention2d_rope_pb_t_kernel(tc, y, wkv, bkv, kn_g, kn_b, out_0, o
                     scale=rstd[c][:, j : j + 1],
                 )
 
-        def apply_gain(u):
-            c, first = place(u)
-            if first == 0:
-                keys[c] = out_pool.tile([P, CHUNK_TILES, KEYS], F32, name="keys")
-            nc.vector.tensor_tensor(
-                out=keys[c][:, first : first + UNIT_TILES, :],
-                in0=xhat[c][:, first : first + UNIT_TILES, :],
-                in1=gain[:],
-                op=ALU.mult,
-            )
-
-        def apply_shift(u):
-            c, first = place(u)
-            nc.vector.tensor_tensor(
-                out=keys[c][:, first : first + UNIT_TILES, :],
-                in0=keys[c][:, first : first + UNIT_TILES, :],
-                in1=shift[:],
-                op=ALU.add,
-            )
-            if first + UNIT_TILES == CHUNK_TILES:
-                nc.sync.dma_start(out=key_chunks[c], in_=keys[c][:].rearrange("p j f -> p (j f)"))
+        def gain_shift_and_store(c):
+            keys[c] = out_pool.tile([P, CHUNK_TILES, KEYS], F32, name="keys")
+            nc.gpsimd.tensor_tensor(out=keys[c][:], in0=xhat[c][:], in1=gain[:], op=ALU.mult)
+            nc.gpsimd.tensor_tensor(out=keys[c][:], in0=keys[c][:], in1=shift[:], op=ALU.add)
+            nc.sync.dma_start(out=key_chunks[c], in_=keys[c][:].rearrange("p j f -> p (j f)"))
 
         def unit_at(step, lag):
             u = step - lag
@@ -257,38 +233,40 @@ def tile_crossattention2d_rope_pb_t_kernel(tc, y, wkv, bkv, kn_g, kn_b, out_0, o
 
         for step in range(N_STEPS):
             c_dev = chunk_at(step, LAG_DEVIATION)
+            u_new = unit_at(step, 0)
+            u_norm = unit_at(step, LAG_NORMALISE)
+            c = chunk_at(step, -CHUNK_UNITS * LOADS_AHEAD)
+            if c is not None:
+                load(c)
             if c_dev is not None:
                 standard_deviation(c_dev)
-            u_new = unit_at(step, 0)
             if u_new is not None:
                 pairs, banks = transpose_and_regroup(u_new)
-                regroup(pairs, banks, 0)
+                regroup(u_new, pairs, banks, 0)
             u = unit_at(step, LAG_PROJECT)
             if u is not None:
                 project(u)
-            u_aff = unit_at(step, LAG_AFFINE)
-            if u_aff is not None:
-                apply_gain(u_aff)
-            u = unit_at(step, LAG_SUM)
-            if u is not None:
-                row_sums(u)
-            u = unit_at(step, LAG_SQUARE)
-            if u is not None:
-                squared_deviations(u)
             u = unit_at(step, LAG_QUANTISE)
             if u is not None:
                 quantise(u)
+            if u_norm is not None:
+                normalise(u_norm, 0)
+            u = unit_at(step, LAG_MOMENTS)
+            if u is not None:
+                moments_of_pairs(u)
             if c_dev is not None:
                 row_factors(c_dev)
+            if step == LAG_BIAS - 1:
+                spread_vectors()
             if u_new is not None:
-                regroup(pairs, banks, 1)
-            if u_aff is not None:
-                apply_shift(u_aff)
+                regroup(u_new, pairs, banks, 1)
             u = unit_at(step, LAG_BIAS)
             if u is not None:
                 add_bias(u)
             if c_dev is not None:
                 row_offsets(c_dev)
-            u = unit_at(step, LAG_NORMALISE)
-            if u is not None:
-                normalise(u)
+            if u_norm is not None:
+                normalise(u_norm, 1)
+            c = chunk_at(step, LAG_AFFINE)
+            if c is not None:
+                gain_shift_and_store(c)

@@ -40,6 +40,8 @@ N_STEPS = N_UNITS + LAG_AFFINE
 
 LOADS_AHEAD = 6
 
+CHUNKS_FINISHED_BY_VECTOR = 2
+
 VECTOR_EVERY = 1000
 
 FLOPS = 2 * ROWS * K * P
@@ -65,40 +67,47 @@ def tile_crossattention2d_rope_pb_t_kernel(tc, y, wkv, bkv, kn_g, kn_b, out_0, o
         words_psum = ctx.enter_context(tc.psum_pool(name="words_psum", bufs=4))
         product_psum = ctx.enter_context(tc.psum_pool(name="product_psum", bufs=4))
 
+        y_tiles = {}
+
+        def load(c, pieces):
+            width = CHUNK_TILES * K // pieces
+            for i in range(pieces):
+                piece = y_pool.tile([P, width], BF16, name="y_%d_%d" % (c, i))
+                nc.sync.dma_start(out=piece[:], in_=y_chunks[c][:, i * width : (i + 1) * width])
+                for j in range(CHUNK_TILES // pieces):
+                    y_tiles[(c, i * (CHUNK_TILES // pieces) + j)] = piece[:, j * K : (j + 1) * K]
+                if c == 0 and i == 0:
+                    nc.sync.dma_start(out=w_rows[:], in_=wkv)
+
         w_rows = consts.tile([P, K], BF16, name="w_rows")
-        nc.sync.dma_start(out=w_rows[:], in_=wkv)
         vectors_bf16 = consts.tile([P, 2 * P], BF16, name="vectors_bf16")
-        y_rows = {}
-
-        def load(c):
-            y_rows[c] = y_pool.tile([P, CHUNK_TILES * K], BF16, name="y_chunk_%d" % c)
-            nc.sync.dma_start(out=y_rows[c][:], in_=y_chunks[c])
-
-        load(0)
+        load(0, CHUNK_TILES // BANK_TILES)
         nc.sync.dma_start(out=vectors_bf16[:, 0:P], in_=bkv.partition_broadcast(P))
         nc.sync.dma_start(out=vectors_bf16[:, P : P + KEYS], in_=kn_g.partition_broadcast(P))
         nc.sync.dma_start(out=vectors_bf16[:, P + KEYS : 2 * P], in_=kn_b.partition_broadcast(P))
         for c in range(1, LOADS_AHEAD):
-            load(c)
+            load(c, 1)
 
         eps = consts.tile([P, 1], F32, name="eps")
         nc.vector.memset(eps[:], EPS)
         table_warmer = consts.tile([P, 1], F32, name="table_warmer")
-        nc.scalar.activation(out=table_warmer[:], in_=eps[:], func=ACT.Sqrt)
+        nc.scalar.activation(out=table_warmer[:], in_=eps[:], func=ACT.Abs_reciprocal_sqrt)
         identity = consts.tile([P, P], F32, name="identity")
         make_identity(nc, identity[:])
 
-        w_words = words_psum.tile([P, 2, P], F32, tag="words", name="w_words")
-        for h in range(2):
-            nc.tensor.transpose(w_words[:, h, :], w_rows[:].bitcast(F32)[:, h : ROW_WORDS : 2], identity[:])
         w_grouped = consts.tile([P, 4 * P], BF16, name="w_grouped", align_bytes=64)
-        nc.vector.tensor_copy(
-            out=w_grouped[:].bitcast(F32).rearrange("p (f h) -> p f h", h=2),
-            in_=w_words[:].rearrange("p h f -> p f h"),
-        )
         w_codes = consts.tile([P, P], U32, name="w_codes", align_bytes=64)
         w_scales = consts.tile([P, P], U8, name="w_scales", align_bytes=64)
-        nc.vector.quantize_mx(out=w_codes[:].bitcast(FP8X4), scales=w_scales[:], in_=w_grouped[:])
+
+        def prepare_weights():
+            w_words = words_psum.tile([P, 2, P], F32, tag="words", name="w_words")
+            for h in range(2):
+                nc.tensor.transpose(w_words[:, h, :], w_rows[:].bitcast(F32)[:, h : ROW_WORDS : 2], identity[:])
+            nc.vector.tensor_copy(
+                out=w_grouped[:].bitcast(F32).rearrange("p (f h) -> p f h", h=2),
+                in_=w_words[:].rearrange("p h f -> p f h"),
+            )
+            nc.vector.quantize_mx(out=w_codes[:].bitcast(FP8X4), scales=w_scales[:], in_=w_grouped[:])
 
         bias = consts.tile([P, UNIT_TILES, P], F32, name="bias")
         gain = consts.tile([P, CHUNK_TILES, KEYS], F32, name="gain")
@@ -117,7 +126,6 @@ def tile_crossattention2d_rope_pb_t_kernel(tc, y, wkv, bkv, kn_g, kn_b, out_0, o
         product = {}
         x = {}
         moments = {}
-        deviation = {}
         rstd = {}
         offset = {}
         xhat = {}
@@ -128,7 +136,6 @@ def tile_crossattention2d_rope_pb_t_kernel(tc, y, wkv, bkv, kn_g, kn_b, out_0, o
 
         def transpose_and_regroup(u):
             c, first = place(u)
-            words = y_rows[c][:].bitcast(F32)
             grouped[u] = grouped_pool.tile([P, 4 * UNIT_ROWS], BF16, name="grouped", align_bytes=64)
             pairs = grouped[u][:].bitcast(F32).rearrange("p (r h) -> p r h", h=2)
             banks = []
@@ -136,11 +143,9 @@ def tile_crossattention2d_rope_pb_t_kernel(tc, y, wkv, bkv, kn_g, kn_b, out_0, o
                 bank = words_psum.tile([P, 2, BANK_ROWS], F32, tag="words", name="bank")
                 banks.append(bank)
                 for i in range(BANK_TILES):
-                    start = (first + b * BANK_TILES + i) * ROW_WORDS
+                    words = y_tiles[(c, first + b * BANK_TILES + i)].bitcast(F32)
                     for h in range(2):
-                        nc.tensor.transpose(
-                            bank[:, h, i * P : (i + 1) * P], words[:, start + h : start + ROW_WORDS : 2], identity[:]
-                        )
+                        nc.tensor.transpose(bank[:, h, i * P : (i + 1) * P], words[:, h : ROW_WORDS : 2], identity[:])
             return pairs, banks
 
         def regroup(u, pairs, banks, b):
@@ -188,15 +193,15 @@ def tile_crossattention2d_rope_pb_t_kernel(tc, y, wkv, bkv, kn_g, kn_b, out_0, o
                     in_=x[c][:, 0, j : j + 2, :].rearrange("p j f -> p f j"),
                 )
 
-        def standard_deviation(c):
-            deviation[c] = stat_pool.tile([P, CHUNK_TILES], F32, name="deviation")
-            nc.scalar.activation(
-                out=deviation[c][:], in_=moments[c][:, :, 2], func=ACT.Sqrt, bias=eps[:, 0:1], scale=1.0 / KEYS
-            )
-
         def row_factors(c):
             rstd[c] = stat_pool.tile([P, CHUNK_TILES], F32, name="rstd")
-            nc.vector.reciprocal(out=rstd[c][:], in_=deviation[c][:])
+            nc.scalar.activation(
+                out=rstd[c][:],
+                in_=moments[c][:, :, 2],
+                func=ACT.Abs_reciprocal_sqrt,
+                bias=eps[:, 0:1],
+                scale=1.0 / KEYS,
+            )
 
         def row_offsets(c):
             offset[c] = stat_pool.tile([P, CHUNK_TILES], F32, name="offset")
@@ -219,8 +224,9 @@ def tile_crossattention2d_rope_pb_t_kernel(tc, y, wkv, bkv, kn_g, kn_b, out_0, o
 
         def gain_shift_and_store(c):
             keys[c] = out_pool.tile([P, CHUNK_TILES, KEYS], F32, name="keys")
-            nc.gpsimd.tensor_tensor(out=keys[c][:], in0=xhat[c][:], in1=gain[:], op=ALU.mult)
-            nc.gpsimd.tensor_tensor(out=keys[c][:], in0=keys[c][:], in1=shift[:], op=ALU.add)
+            engine = nc.vector if c >= N_CHUNKS - CHUNKS_FINISHED_BY_VECTOR else nc.gpsimd
+            engine.tensor_tensor(out=keys[c][:], in0=xhat[c][:], in1=gain[:], op=ALU.mult)
+            engine.tensor_tensor(out=keys[c][:], in0=keys[c][:], in1=shift[:], op=ALU.add)
             nc.sync.dma_start(out=key_chunks[c], in_=keys[c][:].rearrange("p j f -> p (j f)"))
 
         def unit_at(step, lag):
@@ -237,12 +243,14 @@ def tile_crossattention2d_rope_pb_t_kernel(tc, y, wkv, bkv, kn_g, kn_b, out_0, o
             u_norm = unit_at(step, LAG_NORMALISE)
             c = chunk_at(step, -CHUNK_UNITS * LOADS_AHEAD)
             if c is not None:
-                load(c)
+                load(c, 1)
             if c_dev is not None:
-                standard_deviation(c_dev)
+                row_factors(c_dev)
             if u_new is not None:
                 pairs, banks = transpose_and_regroup(u_new)
                 regroup(u_new, pairs, banks, 0)
+            if step == 0:
+                prepare_weights()
             u = unit_at(step, LAG_PROJECT)
             if u is not None:
                 project(u)
@@ -254,8 +262,6 @@ def tile_crossattention2d_rope_pb_t_kernel(tc, y, wkv, bkv, kn_g, kn_b, out_0, o
             u = unit_at(step, LAG_MOMENTS)
             if u is not None:
                 moments_of_pairs(u)
-            if c_dev is not None:
-                row_factors(c_dev)
             if step == LAG_BIAS - 1:
                 spread_vectors()
             if u_new is not None:

@@ -39,6 +39,7 @@ LAG_AFFINE = 9
 N_STEPS = N_UNITS + LAG_AFFINE
 
 LOADS_AHEAD = 6
+CHUNKS_IN_PIECES = 3
 
 CHUNKS_FINISHED_BY_VECTOR = 2
 
@@ -81,11 +82,13 @@ def tile_crossattention2d_rope_pb_t_kernel(tc, y, wkv, bkv, kn_g, kn_b, out_0, o
 
         w_rows = consts.tile([P, K], BF16, name="w_rows")
         vectors_bf16 = consts.tile([P, 2 * P], BF16, name="vectors_bf16")
-        load(0, CHUNK_TILES // BANK_TILES)
-        nc.sync.dma_start(out=vectors_bf16[:, 0:P], in_=bkv.partition_broadcast(P))
+        for c in range(CHUNKS_IN_PIECES):
+            load(c, CHUNK_TILES // BANK_TILES)
+            if c == 0:
+                nc.sync.dma_start(out=vectors_bf16[:, 0:P], in_=bkv.partition_broadcast(P))
         nc.sync.dma_start(out=vectors_bf16[:, P : P + KEYS], in_=kn_g.partition_broadcast(P))
         nc.sync.dma_start(out=vectors_bf16[:, P + KEYS : 2 * P], in_=kn_b.partition_broadcast(P))
-        for c in range(1, LOADS_AHEAD):
+        for c in range(CHUNKS_IN_PIECES, LOADS_AHEAD):
             load(c, 1)
 
         eps = consts.tile([P, 1], F32, name="eps")
@@ -109,16 +112,12 @@ def tile_crossattention2d_rope_pb_t_kernel(tc, y, wkv, bkv, kn_g, kn_b, out_0, o
             )
             nc.vector.quantize_mx(out=w_codes[:].bitcast(FP8X4), scales=w_scales[:], in_=w_grouped[:])
 
-        bias = consts.tile([P, UNIT_TILES, P], F32, name="bias")
-        gain = consts.tile([P, CHUNK_TILES, KEYS], F32, name="gain")
-        shift = consts.tile([P, CHUNK_TILES, KEYS], F32, name="shift")
+        def repeated(vector, n):
+            return vector.unsqueeze(1).to_broadcast([P, n] + list(vector.shape[1:]))
 
-        def spread_vectors():
-            for i in range(UNIT_TILES):
-                nc.vector.tensor_copy(out=bias[:, i, :], in_=vectors_bf16[:, 0:P])
-            for j in range(CHUNK_TILES):
-                nc.gpsimd.tensor_copy(out=gain[:, j, :], in_=vectors_bf16[:, P : P + KEYS])
-                nc.gpsimd.tensor_copy(out=shift[:, j, :], in_=vectors_bf16[:, P + KEYS : 2 * P])
+        bias = vectors_bf16[:, 0:P].rearrange("p (h f) -> p h f", h=2)
+        gain = vectors_bf16[:, P : P + KEYS]
+        shift = vectors_bf16[:, P + KEYS : 2 * P]
 
         grouped = {}
         y_codes = {}
@@ -177,7 +176,7 @@ def tile_crossattention2d_rope_pb_t_kernel(tc, y, wkv, bkv, kn_g, kn_b, out_0, o
             nc.vector.tensor_tensor(
                 out=x[c][:, :, first : first + UNIT_TILES, :].rearrange("p h j f -> p j h f"),
                 in0=product[u][:].rearrange("p j (h f) -> p j h f", h=2),
-                in1=bias[:].rearrange("p j (h f) -> p j h f", h=2),
+                in1=repeated(bias, UNIT_TILES),
                 op=ALU.add,
             )
             if first + UNIT_TILES == CHUNK_TILES:
@@ -225,8 +224,8 @@ def tile_crossattention2d_rope_pb_t_kernel(tc, y, wkv, bkv, kn_g, kn_b, out_0, o
         def gain_shift_and_store(c):
             keys[c] = out_pool.tile([P, CHUNK_TILES, KEYS], F32, name="keys")
             engine = nc.vector if c >= N_CHUNKS - CHUNKS_FINISHED_BY_VECTOR else nc.gpsimd
-            engine.tensor_tensor(out=keys[c][:], in0=xhat[c][:], in1=gain[:], op=ALU.mult)
-            engine.tensor_tensor(out=keys[c][:], in0=keys[c][:], in1=shift[:], op=ALU.add)
+            engine.tensor_tensor(out=keys[c][:], in0=xhat[c][:], in1=repeated(gain, CHUNK_TILES), op=ALU.mult)
+            engine.tensor_tensor(out=keys[c][:], in0=keys[c][:], in1=repeated(shift, CHUNK_TILES), op=ALU.add)
             nc.sync.dma_start(out=key_chunks[c], in_=keys[c][:].rearrange("p j f -> p (j f)"))
 
         def unit_at(step, lag):
@@ -262,8 +261,6 @@ def tile_crossattention2d_rope_pb_t_kernel(tc, y, wkv, bkv, kn_g, kn_b, out_0, o
             u = unit_at(step, LAG_MOMENTS)
             if u is not None:
                 moments_of_pairs(u)
-            if step == LAG_BIAS - 1:
-                spread_vectors()
             if u_new is not None:
                 regroup(u_new, pairs, banks, 1)
             u = unit_at(step, LAG_BIAS)

@@ -27,23 +27,19 @@ UNIT_BANKS = UNIT_TILES // BANK_TILES
 CHUNK_TILES = 8
 CHUNK_UNITS = CHUNK_TILES // UNIT_TILES
 N_CHUNKS = ROWS // (CHUNK_TILES * P)
-N_UNITS = N_CHUNKS * CHUNK_UNITS
 
 LAG_QUANTISE = 1
-LAG_PROJECT = 2
-LAG_BIAS = 3
-LAG_MOMENTS = 4
-LAG_DEVIATION = 6
-LAG_NORMALISE = 7
-LAG_AFFINE = 9
-N_STEPS = N_UNITS + LAG_AFFINE
+LAG_PROJECT = 1
+LAG_BIAS = 2
+LAG_NORMALISE = 3
+LAG_GAIN = 4
+LAG_SHIFT = 5
+N_STEPS = N_CHUNKS + LAG_SHIFT
 
 LOADS_AHEAD = 6
 CHUNKS_IN_PIECES = 3
 
 CHUNKS_FINISHED_BY_VECTOR = 2
-
-VECTOR_EVERY = 1000
 
 FLOPS = 2 * ROWS * K * P
 
@@ -63,6 +59,7 @@ def tile_crossattention2d_rope_pb_t_kernel(tc, y, wkv, bkv, kn_g, kn_b, out_0, o
         codes_pool = ctx.enter_context(tc.tile_pool(name="codes_pool", bufs=4))
         x_pool = ctx.enter_context(tc.tile_pool(name="x_pool", bufs=6))
         stat_pool = ctx.enter_context(tc.tile_pool(name="stat_pool", bufs=6))
+        scaled_pool = ctx.enter_context(tc.tile_pool(name="scaled_pool", bufs=1))
         xhat_pool = ctx.enter_context(tc.tile_pool(name="xhat_pool", bufs=4))
         out_pool = ctx.enter_context(tc.tile_pool(name="out_pool", bufs=4))
         words_psum = ctx.enter_context(tc.psum_pool(name="words_psum", bufs=4))
@@ -128,28 +125,25 @@ def tile_crossattention2d_rope_pb_t_kernel(tc, y, wkv, bkv, kn_g, kn_b, out_0, o
         rstd = {}
         offset = {}
         xhat = {}
-        keys = {}
+        scaled = {}
 
         def place(u):
             return u // CHUNK_UNITS, (u % CHUNK_UNITS) * UNIT_TILES
+
+        def units(c):
+            return range(c * CHUNK_UNITS, (c + 1) * CHUNK_UNITS)
 
         def transpose_and_regroup(u):
             c, first = place(u)
             grouped[u] = grouped_pool.tile([P, 4 * UNIT_ROWS], BF16, name="grouped", align_bytes=64)
             pairs = grouped[u][:].bitcast(F32).rearrange("p (r h) -> p r h", h=2)
-            banks = []
             for b in range(UNIT_BANKS):
                 bank = words_psum.tile([P, 2, BANK_ROWS], F32, tag="words", name="bank")
-                banks.append(bank)
                 for i in range(BANK_TILES):
                     words = y_tiles[(c, first + b * BANK_TILES + i)].bitcast(F32)
                     for h in range(2):
                         nc.tensor.transpose(bank[:, h, i * P : (i + 1) * P], words[:, h : ROW_WORDS : 2], identity[:])
-            return pairs, banks
-
-        def regroup(u, pairs, banks, b):
-            engine = nc.vector.tensor_copy if (u * UNIT_BANKS + b) % VECTOR_EVERY == VECTOR_EVERY - 1 else nc.scalar.copy
-            engine(out=pairs[:, b * BANK_ROWS : (b + 1) * BANK_ROWS, :], in_=banks[b][:].rearrange("p h r -> p r h"))
+                nc.scalar.copy(out=pairs[:, b * BANK_ROWS : (b + 1) * BANK_ROWS, :], in_=bank[:].rearrange("p h r -> p r h"))
 
         def quantise(u):
             y_codes[u] = codes_pool.tile([P, UNIT_ROWS], U32, name="y_codes", align_bytes=64)
@@ -208,11 +202,11 @@ def tile_crossattention2d_rope_pb_t_kernel(tc, y, wkv, bkv, kn_g, kn_b, out_0, o
                 out=offset[c][:], in0=moments[c][:, :, 1], scalar=-1.0, in1=rstd[c][:], op0=ALU.mult, op1=ALU.mult
             )
 
-        def normalise(u, half):
+        def normalise(u):
             c, first = place(u)
-            if first == 0 and half == 0:
+            if first == 0:
                 xhat[c] = xhat_pool.tile([P, CHUNK_TILES, KEYS], F32, name="xhat")
-            for j in range(first + 2 * half, first + 2 * half + 2):
+            for j in range(first, first + UNIT_TILES):
                 nc.scalar.activation(
                     out=xhat[c][:, j, :],
                     in_=x[c][:, 0, j, :],
@@ -221,55 +215,55 @@ def tile_crossattention2d_rope_pb_t_kernel(tc, y, wkv, bkv, kn_g, kn_b, out_0, o
                     scale=rstd[c][:, j : j + 1],
                 )
 
-        def gain_shift_and_store(c):
-            keys[c] = out_pool.tile([P, CHUNK_TILES, KEYS], F32, name="keys")
+        def apply_gain(c):
+            scaled[c] = scaled_pool.tile([P, CHUNK_TILES, KEYS], F32, name="scaled")
             engine = nc.vector if c >= N_CHUNKS - CHUNKS_FINISHED_BY_VECTOR else nc.gpsimd
-            engine.tensor_tensor(out=keys[c][:], in0=xhat[c][:], in1=repeated(gain, CHUNK_TILES), op=ALU.mult)
-            engine.tensor_tensor(out=keys[c][:], in0=keys[c][:], in1=repeated(shift, CHUNK_TILES), op=ALU.add)
-            nc.sync.dma_start(out=key_chunks[c], in_=keys[c][:].rearrange("p j f -> p (j f)"))
+            engine.tensor_tensor(out=scaled[c][:], in0=xhat[c][:], in1=repeated(gain, CHUNK_TILES), op=ALU.mult)
 
-        def unit_at(step, lag):
-            u = step - lag
-            return u if 0 <= u < N_UNITS else None
+        def shift_and_store(c):
+            keys = out_pool.tile([P, CHUNK_TILES, KEYS], F32, name="keys")
+            nc.vector.tensor_tensor(out=keys[:], in0=scaled[c][:], in1=repeated(shift, CHUNK_TILES), op=ALU.add)
+            nc.sync.dma_start(out=key_chunks[c], in_=keys[:].rearrange("p j f -> p (j f)"))
 
         def chunk_at(step, lag):
-            u = step - lag
-            return u // CHUNK_UNITS if 0 <= u < N_UNITS and u % CHUNK_UNITS == 0 else None
+            c = step - lag
+            return c if 0 <= c < N_CHUNKS else None
 
         for step in range(N_STEPS):
-            c_dev = chunk_at(step, LAG_DEVIATION)
-            u_new = unit_at(step, 0)
-            u_norm = unit_at(step, LAG_NORMALISE)
-            c = chunk_at(step, -CHUNK_UNITS * LOADS_AHEAD)
+            c = chunk_at(step, -LOADS_AHEAD)
             if c is not None:
                 load(c, 1)
-            if c_dev is not None:
-                row_factors(c_dev)
-            if u_new is not None:
-                pairs, banks = transpose_and_regroup(u_new)
-                regroup(u_new, pairs, banks, 0)
-            if step == 0:
-                prepare_weights()
-            u = unit_at(step, LAG_PROJECT)
-            if u is not None:
-                project(u)
-            u = unit_at(step, LAG_QUANTISE)
-            if u is not None:
-                quantise(u)
-            if u_norm is not None:
-                normalise(u_norm, 0)
-            u = unit_at(step, LAG_MOMENTS)
-            if u is not None:
-                moments_of_pairs(u)
-            if u_new is not None:
-                regroup(u_new, pairs, banks, 1)
-            u = unit_at(step, LAG_BIAS)
-            if u is not None:
-                add_bias(u)
-            if c_dev is not None:
-                row_offsets(c_dev)
-            if u_norm is not None:
-                normalise(u_norm, 1)
-            c = chunk_at(step, LAG_AFFINE)
+            c = chunk_at(step, LAG_QUANTISE)
             if c is not None:
-                gain_shift_and_store(c)
+                for u in units(c):
+                    quantise(u)
+            c = chunk_at(step, LAG_NORMALISE)
+            if c is not None:
+                row_offsets(c)
+            c = chunk_at(step, LAG_SHIFT)
+            if c is not None:
+                shift_and_store(c)
+            c = chunk_at(step, LAG_GAIN)
+            if c is not None:
+                apply_gain(c)
+            c = chunk_at(step, 0)
+            if c is not None:
+                for u in units(c):
+                    transpose_and_regroup(u)
+                    if u == 0:
+                        prepare_weights()
+            c = chunk_at(step, LAG_PROJECT)
+            if c is not None:
+                for u in units(c):
+                    project(u)
+            c = chunk_at(step, LAG_NORMALISE)
+            if c is not None:
+                for u in units(c):
+                    normalise(u)
+            c = chunk_at(step, LAG_BIAS)
+            if c is not None:
+                for u in units(c):
+                    add_bias(u)
+                for u in units(c):
+                    moments_of_pairs(u)
+                row_factors(c)

@@ -34,12 +34,13 @@ LAG_BIAS = 2
 LAG_NORMALISE = 3
 LAG_GAIN = 4
 LAG_SHIFT = 5
-N_STEPS = N_CHUNKS + LAG_SHIFT
+N_STEPS = N_CHUNKS + LAG_GAIN
 
 LOADS_AHEAD = 6
 CHUNKS_IN_PIECES = 3
 
 CHUNKS_FINISHED_BY_VECTOR = 2
+CHUNKS_FINISHED_BY_GPSIMD = 2
 
 FLOPS = 2 * ROWS * K * P
 
@@ -126,6 +127,7 @@ def tile_crossattention2d_rope_pb_t_kernel(tc, y, wkv, bkv, kn_g, kn_b, out_0, o
         offset = {}
         xhat = {}
         scaled = {}
+        keys = {}
 
         def place(u):
             return u // CHUNK_UNITS, (u % CHUNK_UNITS) * UNIT_TILES
@@ -202,32 +204,51 @@ def tile_crossattention2d_rope_pb_t_kernel(tc, y, wkv, bkv, kn_g, kn_b, out_0, o
                 out=offset[c][:], in0=moments[c][:, :, 1], scalar=-1.0, in1=rstd[c][:], op0=ALU.mult, op1=ALU.mult
             )
 
-        def normalise(u):
-            c, first = place(u)
-            if first == 0:
-                xhat[c] = xhat_pool.tile([P, CHUNK_TILES, KEYS], F32, name="xhat")
-            for j in range(first, first + UNIT_TILES):
-                nc.scalar.activation(
-                    out=xhat[c][:, j, :],
-                    in_=x[c][:, 0, j, :],
-                    func=ACT.Identity,
-                    bias=offset[c][:, j : j + 1],
-                    scale=rstd[c][:, j : j + 1],
-                )
+        def normalise(c, tiles, on_scalar=True):
+            for j in tiles:
+                if on_scalar:
+                    nc.scalar.activation(
+                        out=xhat[c][:, j, :],
+                        in_=x[c][:, 0, j, :],
+                        func=ACT.Identity,
+                        bias=offset[c][:, j : j + 1],
+                        scale=rstd[c][:, j : j + 1],
+                    )
+                else:
+                    nc.vector.tensor_scalar(
+                        out=xhat[c][:, j, :],
+                        in0=x[c][:, 0, j, :],
+                        scalar1=rstd[c][:, j : j + 1],
+                        scalar2=offset[c][:, j : j + 1],
+                        op0=ALU.mult,
+                        op1=ALU.add,
+                    )
 
-        def apply_gain(c):
-            scaled[c] = scaled_pool.tile([P, CHUNK_TILES, KEYS], F32, name="scaled")
-            engine = nc.vector if c >= N_CHUNKS - CHUNKS_FINISHED_BY_VECTOR else nc.gpsimd
-            engine.tensor_tensor(out=scaled[c][:], in0=xhat[c][:], in1=repeated(gain, CHUNK_TILES), op=ALU.mult)
+        def apply_gain(c, engine, pool, tiles=slice(0, CHUNK_TILES)):
+            n = tiles.stop - tiles.start
+            if tiles.start == 0:
+                scaled[c] = pool.tile([P, CHUNK_TILES, KEYS], F32, name="scaled")
+            engine.tensor_tensor(out=scaled[c][:, tiles, :], in0=xhat[c][:, tiles, :], in1=repeated(gain, n), op=ALU.mult)
 
-        def shift_and_store(c):
-            keys = out_pool.tile([P, CHUNK_TILES, KEYS], F32, name="keys")
-            nc.vector.tensor_tensor(out=keys[:], in0=scaled[c][:], in1=repeated(shift, CHUNK_TILES), op=ALU.add)
-            nc.sync.dma_start(out=key_chunks[c], in_=keys[:].rearrange("p j f -> p (j f)"))
+        def shift_and_store(c, engine, tiles=slice(0, CHUNK_TILES)):
+            n = tiles.stop - tiles.start
+            if tiles.start == 0:
+                keys[c] = out_pool.tile([P, CHUNK_TILES, KEYS], F32, name="keys")
+            engine.tensor_tensor(out=keys[c][:, tiles, :], in0=scaled[c][:, tiles, :], in1=repeated(shift, n), op=ALU.add)
+            nc.sync.dma_start(
+                out=key_chunks[c][:, tiles.start * KEYS : tiles.stop * KEYS],
+                in_=keys[c][:, tiles, :].rearrange("p j f -> p (j f)"),
+            )
 
         def chunk_at(step, lag):
             c = step - lag
             return c if 0 <= c < N_CHUNKS else None
+
+        ALL = range(CHUNK_TILES)
+        FIRST = slice(0, UNIT_TILES)
+        SECOND = slice(UNIT_TILES, CHUNK_TILES)
+        by_vector = range(N_CHUNKS - CHUNKS_FINISHED_BY_VECTOR, N_CHUNKS)
+        by_gpsimd = range(by_vector.start - CHUNKS_FINISHED_BY_GPSIMD, by_vector.start)
 
         for step in range(N_STEPS):
             c = chunk_at(step, -LOADS_AHEAD)
@@ -241,11 +262,14 @@ def tile_crossattention2d_rope_pb_t_kernel(tc, y, wkv, bkv, kn_g, kn_b, out_0, o
             if c is not None:
                 row_offsets(c)
             c = chunk_at(step, LAG_SHIFT)
-            if c is not None:
-                shift_and_store(c)
+            if c is not None and c < by_gpsimd.start:
+                shift_and_store(c, nc.vector)
             c = chunk_at(step, LAG_GAIN)
-            if c is not None:
-                apply_gain(c)
+            if c is not None and c < by_gpsimd.start:
+                apply_gain(c, nc.gpsimd, scaled_pool)
+            elif c in by_gpsimd:
+                apply_gain(c, nc.gpsimd, out_pool)
+                shift_and_store(c, nc.gpsimd)
             c = chunk_at(step, 0)
             if c is not None:
                 for u in units(c):
@@ -258,8 +282,12 @@ def tile_crossattention2d_rope_pb_t_kernel(tc, y, wkv, bkv, kn_g, kn_b, out_0, o
                     project(u)
             c = chunk_at(step, LAG_NORMALISE)
             if c is not None:
-                for u in units(c):
-                    normalise(u)
+                xhat[c] = xhat_pool.tile([P, CHUNK_TILES, KEYS], F32, name="xhat")
+                if c == N_CHUNKS - 1:
+                    normalise(c, ALL[SECOND], on_scalar=False)
+                    normalise(c, ALL[FIRST])
+                else:
+                    normalise(c, ALL)
             c = chunk_at(step, LAG_BIAS)
             if c is not None:
                 for u in units(c):
@@ -267,3 +295,9 @@ def tile_crossattention2d_rope_pb_t_kernel(tc, y, wkv, bkv, kn_g, kn_b, out_0, o
                 for u in units(c):
                     moments_of_pairs(u)
                 row_factors(c)
+            c = chunk_at(step, LAG_NORMALISE)
+            if c in by_vector:
+                for half in (FIRST, SECOND):
+                    apply_gain(c, nc.vector, out_pool, half)
+                for half in (FIRST, SECOND):
+                    shift_and_store(c, nc.vector, half)

@@ -28,19 +28,13 @@ CHUNK_TILES = 8
 CHUNK_UNITS = CHUNK_TILES // UNIT_TILES
 N_CHUNKS = ROWS // (CHUNK_TILES * P)
 
-LAG_QUANTISE = 1
-LAG_PROJECT = 1
-LAG_BIAS = 2
 LAG_NORMALISE = 3
-LAG_GAIN = 4
-LAG_SHIFT = 5
-N_STEPS = N_CHUNKS + LAG_GAIN
+N_UNITS = N_CHUNKS * CHUNK_UNITS
+OPENING_UNITS = 4
+CHUNK_BANKS = CHUNK_UNITS * UNIT_BANKS
 
 LOADS_AHEAD = 6
 CHUNKS_IN_PIECES = 3
-
-CHUNKS_FINISHED_BY_VECTOR = 2
-CHUNKS_FINISHED_BY_GPSIMD = 2
 
 FLOPS = 2 * ROWS * K * P
 
@@ -69,25 +63,26 @@ def tile_crossattention2d_rope_pb_t_kernel(tc, y, wkv, bkv, kn_g, kn_b, out_0, o
         y_tiles = {}
 
         def load(c, pieces):
-            width = CHUNK_TILES * K // pieces
-            for i in range(pieces):
-                piece = y_pool.tile([P, width], BF16, name="y_%d_%d" % (c, i))
-                nc.sync.dma_start(out=piece[:], in_=y_chunks[c][:, i * width : (i + 1) * width])
-                for j in range(CHUNK_TILES // pieces):
-                    y_tiles[(c, i * (CHUNK_TILES // pieces) + j)] = piece[:, j * K : (j + 1) * K]
-                if c == 0 and i == 0:
+            start = 0
+            for i, tiles in enumerate(pieces):
+                piece = y_pool.tile([P, tiles * K], BF16, name="y_%d_%d" % (c, start))
+                nc.sync.dma_start(out=piece[:], in_=y_chunks[c][:, start * K : (start + tiles) * K])
+                for j in range(tiles):
+                    y_tiles[(c, start + j)] = piece[:, j * K : (j + 1) * K]
+                start += tiles
+                if c == 0 and i == 1:
                     nc.sync.dma_start(out=w_rows[:], in_=wkv)
 
         w_rows = consts.tile([P, K], BF16, name="w_rows")
         vectors_bf16 = consts.tile([P, 2 * P], BF16, name="vectors_bf16")
         for c in range(CHUNKS_IN_PIECES):
-            load(c, CHUNK_TILES // BANK_TILES)
+            load(c, [2,2,2,2] if c == 0 else [BANK_TILES] * (CHUNK_TILES // BANK_TILES))
             if c == 0:
                 nc.sync.dma_start(out=vectors_bf16[:, 0:P], in_=bkv.partition_broadcast(P))
         nc.sync.dma_start(out=vectors_bf16[:, P : P + KEYS], in_=kn_g.partition_broadcast(P))
         nc.sync.dma_start(out=vectors_bf16[:, P + KEYS : 2 * P], in_=kn_b.partition_broadcast(P))
         for c in range(CHUNKS_IN_PIECES, LOADS_AHEAD):
-            load(c, 1)
+            load(c, [CHUNK_TILES])
 
         eps = consts.tile([P, 1], F32, name="eps")
         nc.vector.memset(eps[:], EPS)
@@ -135,17 +130,20 @@ def tile_crossattention2d_rope_pb_t_kernel(tc, y, wkv, bkv, kn_g, kn_b, out_0, o
         def units(c):
             return range(c * CHUNK_UNITS, (c + 1) * CHUNK_UNITS)
 
-        def transpose_and_regroup(u):
+        def transpose_and_regroup(b):
+            u, half = b // UNIT_BANKS, b % UNIT_BANKS
             c, first = place(u)
-            grouped[u] = grouped_pool.tile([P, 4 * UNIT_ROWS], BF16, name="grouped", align_bytes=64)
+            if half == 0:
+                grouped[u] = grouped_pool.tile([P, 4 * UNIT_ROWS], BF16, name="grouped", align_bytes=64)
             pairs = grouped[u][:].bitcast(F32).rearrange("p (r h) -> p r h", h=2)
-            for b in range(UNIT_BANKS):
-                bank = words_psum.tile([P, 2, BANK_ROWS], F32, tag="words", name="bank")
-                for i in range(BANK_TILES):
-                    words = y_tiles[(c, first + b * BANK_TILES + i)].bitcast(F32)
-                    for h in range(2):
-                        nc.tensor.transpose(bank[:, h, i * P : (i + 1) * P], words[:, h : ROW_WORDS : 2], identity[:])
-                nc.scalar.copy(out=pairs[:, b * BANK_ROWS : (b + 1) * BANK_ROWS, :], in_=bank[:].rearrange("p h r -> p r h"))
+            bank = words_psum.tile([P, 2, BANK_ROWS], F32, tag="words", name="bank")
+            for i in range(BANK_TILES):
+                words = y_tiles[(c, first + half * BANK_TILES + i)].bitcast(F32)
+                for h in range(2):
+                    nc.tensor.transpose(bank[:, h, i * P : (i + 1) * P], words[:, h : ROW_WORDS : 2], identity[:])
+            nc.scalar.copy(
+                out=pairs[:, half * BANK_ROWS : (half + 1) * BANK_ROWS, :], in_=bank[:].rearrange("p h r -> p r h")
+            )
 
         def quantise(u):
             y_codes[u] = codes_pool.tile([P, UNIT_ROWS], U32, name="y_codes", align_bytes=64)
@@ -205,7 +203,9 @@ def tile_crossattention2d_rope_pb_t_kernel(tc, y, wkv, bkv, kn_g, kn_b, out_0, o
             )
 
         def normalise(c, tiles, on_scalar=True):
-            for j in tiles:
+            if c not in xhat:
+                xhat[c] = xhat_pool.tile([P, CHUNK_TILES, KEYS], F32, name="xhat")
+            for j in range(tiles.start, tiles.stop):
                 if on_scalar:
                     nc.scalar.activation(
                         out=xhat[c][:, j, :],
@@ -230,74 +230,95 @@ def tile_crossattention2d_rope_pb_t_kernel(tc, y, wkv, bkv, kn_g, kn_b, out_0, o
                 scaled[c] = pool.tile([P, CHUNK_TILES, KEYS], F32, name="scaled")
             engine.tensor_tensor(out=scaled[c][:, tiles, :], in0=xhat[c][:, tiles, :], in1=repeated(gain, n), op=ALU.mult)
 
-        def shift_and_store(c, engine, tiles=slice(0, CHUNK_TILES)):
+        def shift_keys(c, engine, tiles):
             n = tiles.stop - tiles.start
-            if tiles.start == 0:
+            if c not in keys:
                 keys[c] = out_pool.tile([P, CHUNK_TILES, KEYS], F32, name="keys")
             engine.tensor_tensor(out=keys[c][:, tiles, :], in0=scaled[c][:, tiles, :], in1=repeated(shift, n), op=ALU.add)
+
+        def store_keys(c, tiles=slice(0, CHUNK_TILES)):
             nc.sync.dma_start(
                 out=key_chunks[c][:, tiles.start * KEYS : tiles.stop * KEYS],
                 in_=keys[c][:, tiles, :].rearrange("p j f -> p (j f)"),
             )
 
-        def chunk_at(step, lag):
-            c = step - lag
-            return c if 0 <= c < N_CHUNKS else None
+        def shift_and_store(c, engine, tiles=slice(0, CHUNK_TILES)):
+            shift_keys(c, engine, tiles)
+            store_keys(c, tiles)
 
-        ALL = range(CHUNK_TILES)
         FIRST = slice(0, UNIT_TILES)
         SECOND = slice(UNIT_TILES, CHUNK_TILES)
-        by_vector = range(N_CHUNKS - CHUNKS_FINISHED_BY_VECTOR, N_CHUNKS)
-        by_gpsimd = range(by_vector.start - CHUNKS_FINISHED_BY_GPSIMD, by_vector.start)
+        LAST = N_CHUNKS - 1
 
-        for step in range(N_STEPS):
-            c = chunk_at(step, -LOADS_AHEAD)
-            if c is not None:
-                load(c, 1)
-            c = chunk_at(step, LAG_QUANTISE)
-            if c is not None:
-                for u in units(c):
-                    quantise(u)
-            c = chunk_at(step, LAG_NORMALISE)
-            if c is not None:
-                row_offsets(c)
-            c = chunk_at(step, LAG_SHIFT)
-            if c is not None and c < by_gpsimd.start:
-                shift_and_store(c, nc.vector)
-            c = chunk_at(step, LAG_GAIN)
-            if c is not None and c < by_gpsimd.start:
-                apply_gain(c, nc.gpsimd, scaled_pool)
-            elif c in by_gpsimd:
-                apply_gain(c, nc.gpsimd, out_pool)
-                shift_and_store(c, nc.gpsimd)
-            c = chunk_at(step, 0)
-            if c is not None:
-                for u in units(c):
-                    transpose_and_regroup(u)
-                    if u == 0:
-                        prepare_weights()
-            c = chunk_at(step, LAG_PROJECT)
-            if c is not None:
-                for u in units(c):
-                    project(u)
-            c = chunk_at(step, LAG_NORMALISE)
-            if c is not None:
-                xhat[c] = xhat_pool.tile([P, CHUNK_TILES, KEYS], F32, name="xhat")
-                if c == N_CHUNKS - 1:
-                    normalise(c, ALL[SECOND], on_scalar=False)
-                    normalise(c, ALL[FIRST])
-                else:
-                    normalise(c, ALL)
-            c = chunk_at(step, LAG_BIAS)
-            if c is not None:
-                for u in units(c):
-                    add_bias(u)
-                for u in units(c):
-                    moments_of_pairs(u)
+        done = {}
+
+        def advance(stage, n):
+            n = min(n, N_CHUNKS * (CHUNK_BANKS if stage == transpose_and_regroup else CHUNK_UNITS))
+            for item in range(done.get(stage, 0), n):
+                stage(item)
+            done[stage] = max(done.get(stage, 0), n)
+
+        advance(transpose_and_regroup, UNIT_BANKS)
+        prepare_weights()
+        for u in range(1, OPENING_UNITS):
+            if u % CHUNK_UNITS == 0:
+                load(LOADS_AHEAD + u // CHUNK_UNITS - 1, [CHUNK_TILES])
+            advance(transpose_and_regroup, (u + 1) * UNIT_BANKS)
+            advance(quantise, u)
+            advance(project, u - 1)
+            advance(add_bias, u - 1)
+            advance(moments_of_pairs, u - 2)
+
+        for step in range(OPENING_UNITS // CHUNK_UNITS, N_CHUNKS):
+            if step + LOADS_AHEAD - 1 < N_CHUNKS:
+                load(step + LOADS_AHEAD - 1, [CHUNK_TILES])
+            c = step - LAG_NORMALISE
+            advance(quantise, step * CHUNK_UNITS - 1)
+            if c >= 0:
                 row_factors(c)
-            c = chunk_at(step, LAG_NORMALISE)
-            if c in by_vector:
-                for half in (FIRST, SECOND):
-                    apply_gain(c, nc.vector, out_pool, half)
-                for half in (FIRST, SECOND):
-                    shift_and_store(c, nc.vector, half)
+                row_offsets(c)
+            advance(quantise, step * CHUNK_UNITS)
+            if c >= 1:
+                shift_keys(c - 1, nc.vector, slice(0, CHUNK_TILES - 2))
+                store_keys(c - 1)
+            advance(transpose_and_regroup, step * CHUNK_BANKS + 1)
+            if c >= 0:
+                normalise(c, FIRST)
+                normalise(c, SECOND)
+                apply_gain(c, nc.gpsimd, scaled_pool)
+                shift_keys(c, nc.gpsimd, slice(CHUNK_TILES - 2, CHUNK_TILES))
+            advance(transpose_and_regroup, (step + 1) * CHUNK_BANKS)
+            advance(project, step * CHUNK_UNITS)
+            advance(add_bias, (step - 1) * CHUNK_UNITS)
+            advance(moments_of_pairs, (step - 1) * CHUNK_UNITS)
+
+        advance(quantise, N_UNITS)
+        row_factors(LAST - 2)
+        row_offsets(LAST - 2)
+        shift_keys(LAST - 3, nc.vector, slice(0, CHUNK_TILES - 2))
+        store_keys(LAST - 3)
+        normalise(LAST - 2, FIRST)
+        normalise(LAST - 2, SECOND)
+        apply_gain(LAST - 2, nc.gpsimd, out_pool)
+        shift_and_store(LAST - 2, nc.gpsimd)
+        advance(project, N_UNITS)
+        advance(add_bias, N_UNITS - CHUNK_UNITS)
+        advance(moments_of_pairs, N_UNITS - CHUNK_UNITS)
+        row_factors(LAST - 1)
+        advance(add_bias, N_UNITS)
+        row_offsets(LAST - 1)
+        advance(moments_of_pairs, N_UNITS)
+        normalise(LAST - 1, FIRST)
+        normalise(LAST - 1, SECOND)
+        row_factors(LAST)
+        for half in (FIRST, SECOND):
+            apply_gain(LAST - 1, nc.vector, out_pool, half)
+        row_offsets(LAST)
+        normalise(LAST, FIRST)
+        normalise(LAST, SECOND)
+        for half in (FIRST, SECOND):
+            shift_and_store(LAST - 1, nc.vector, half)
+        for half in (FIRST, SECOND):
+            apply_gain(LAST, nc.vector, out_pool, half)
+        for half in (FIRST, SECOND):
+            shift_and_store(LAST, nc.vector, half)

@@ -34,7 +34,7 @@ OPENING_UNITS = 4
 CHUNK_BANKS = CHUNK_UNITS * UNIT_BANKS
 
 LOADS_AHEAD = 6
-CHUNKS_IN_PIECES = 3
+CHUNKS_IN_PIECES = 4
 
 FLOPS = 2 * ROWS * K * P
 
@@ -226,7 +226,7 @@ def tile_crossattention2d_rope_pb_t_kernel(tc, y, wkv, bkv, kn_g, kn_b, out_0, o
 
         def apply_gain(c, engine, pool, tiles=slice(0, CHUNK_TILES)):
             n = tiles.stop - tiles.start
-            if tiles.start == 0:
+            if c not in scaled:
                 scaled[c] = pool.tile([P, CHUNK_TILES, KEYS], F32, name="scaled")
             engine.tensor_tensor(out=scaled[c][:, tiles, :], in0=xhat[c][:, tiles, :], in1=repeated(gain, n), op=ALU.mult)
 
@@ -248,6 +248,7 @@ def tile_crossattention2d_rope_pb_t_kernel(tc, y, wkv, bkv, kn_g, kn_b, out_0, o
 
         FIRST = slice(0, UNIT_TILES)
         SECOND = slice(UNIT_TILES, CHUNK_TILES)
+        ALL = slice(0, CHUNK_TILES)
         LAST = N_CHUNKS - 1
 
         done = {}
@@ -279,46 +280,48 @@ def tile_crossattention2d_rope_pb_t_kernel(tc, y, wkv, bkv, kn_g, kn_b, out_0, o
                 row_offsets(c)
             advance(quantise, step * CHUNK_UNITS)
             if c >= 1:
-                shift_keys(c - 1, nc.vector, slice(0, CHUNK_TILES - 2))
+                shift_keys(c - 1, nc.vector, ALL)
                 store_keys(c - 1)
             advance(transpose_and_regroup, step * CHUNK_BANKS + 1)
             if c >= 0:
-                normalise(c, FIRST)
-                normalise(c, SECOND)
+                normalise(c, ALL)
+            if c >= 1:
                 apply_gain(c, nc.gpsimd, scaled_pool)
-                shift_keys(c, nc.gpsimd, slice(CHUNK_TILES - 2, CHUNK_TILES))
             advance(transpose_and_regroup, (step + 1) * CHUNK_BANKS)
             advance(project, step * CHUNK_UNITS)
             advance(add_bias, (step - 1) * CHUNK_UNITS)
             advance(moments_of_pairs, (step - 1) * CHUNK_UNITS)
+            if c == 0:
+                apply_gain(c, nc.vector, scaled_pool)
 
         advance(quantise, N_UNITS)
         row_factors(LAST - 2)
         row_offsets(LAST - 2)
-        shift_keys(LAST - 3, nc.vector, slice(0, CHUNK_TILES - 2))
+        shift_keys(LAST - 3, nc.vector, ALL)
         store_keys(LAST - 3)
-        normalise(LAST - 2, FIRST)
-        normalise(LAST - 2, SECOND)
+        normalise(LAST - 2, ALL)
         apply_gain(LAST - 2, nc.gpsimd, out_pool)
-        shift_and_store(LAST - 2, nc.gpsimd)
         advance(project, N_UNITS)
         advance(add_bias, N_UNITS - CHUNK_UNITS)
         advance(moments_of_pairs, N_UNITS - CHUNK_UNITS)
         row_factors(LAST - 1)
-        advance(add_bias, N_UNITS)
+        advance(add_bias, N_UNITS - 1)
         row_offsets(LAST - 1)
+        advance(add_bias, N_UNITS)
+        normalise(LAST - 1, ALL)
         advance(moments_of_pairs, N_UNITS)
-        normalise(LAST - 1, FIRST)
-        normalise(LAST - 1, SECOND)
         row_factors(LAST)
+        shift_keys(LAST - 2, nc.vector, ALL)
+        store_keys(LAST - 2)
+        row_offsets(LAST)
+        normalise(LAST, ALL)
         for half in (FIRST, SECOND):
             apply_gain(LAST - 1, nc.vector, out_pool, half)
-        row_offsets(LAST)
-        normalise(LAST, FIRST)
-        normalise(LAST, SECOND)
         for half in (FIRST, SECOND):
-            shift_and_store(LAST - 1, nc.vector, half)
+            shift_keys(LAST - 1, nc.vector, half)
+        store_keys(LAST - 1)
         for half in (FIRST, SECOND):
             apply_gain(LAST, nc.vector, out_pool, half)
         for half in (FIRST, SECOND):
-            shift_and_store(LAST, nc.vector, half)
+            shift_keys(LAST, nc.vector, half)
+            store_keys(LAST, half)

@@ -186,20 +186,27 @@ def tile_crossattention2d_rope_pb_t_kernel(tc, y, wkv, bkv, kn_g, kn_b, out_0, o
                     in_=x[c][:, 0, j : j + 2, :].rearrange("p j f -> p f j"),
                 )
 
-        def row_factors(c):
-            rstd[c] = stat_pool.tile([P, CHUNK_TILES], F32, name="rstd")
+        def row_factors(c, tiles):
+            if c not in rstd:
+                rstd[c] = stat_pool.tile([P, CHUNK_TILES], F32, name="rstd")
             nc.scalar.activation(
-                out=rstd[c][:],
-                in_=moments[c][:, :, 2],
+                out=rstd[c][:, tiles],
+                in_=moments[c][:, tiles, 2],
                 func=ACT.Abs_reciprocal_sqrt,
                 bias=eps[:, 0:1],
                 scale=1.0 / KEYS,
             )
 
-        def row_offsets(c):
-            offset[c] = stat_pool.tile([P, CHUNK_TILES], F32, name="offset")
+        def row_offsets(c, tiles):
+            if c not in offset:
+                offset[c] = stat_pool.tile([P, CHUNK_TILES], F32, name="offset")
             nc.vector.scalar_tensor_tensor(
-                out=offset[c][:], in0=moments[c][:, :, 1], scalar=-1.0, in1=rstd[c][:], op0=ALU.mult, op1=ALU.mult
+                out=offset[c][:, tiles],
+                in0=moments[c][:, tiles, 1],
+                scalar=-1.0,
+                in1=rstd[c][:, tiles],
+                op0=ALU.mult,
+                op1=ALU.mult,
             )
 
         def normalise(c, tiles, on_scalar=True):
@@ -246,80 +253,77 @@ def tile_crossattention2d_rope_pb_t_kernel(tc, y, wkv, bkv, kn_g, kn_b, out_0, o
             shift_keys(c, engine, tiles)
             store_keys(c, tiles)
 
+        ALL = slice(0, CHUNK_TILES)
         FIRST = slice(0, UNIT_TILES)
         SECOND = slice(UNIT_TILES, CHUNK_TILES)
-        ALL = slice(0, CHUNK_TILES)
         LAST = N_CHUNKS - 1
 
-        done = {}
-
-        def advance(stage, n):
-            n = min(n, N_CHUNKS * (CHUNK_BANKS if stage == transpose_and_regroup else CHUNK_UNITS))
-            for item in range(done.get(stage, 0), n):
-                stage(item)
-            done[stage] = max(done.get(stage, 0), n)
-
-        advance(transpose_and_regroup, UNIT_BANKS)
-        prepare_weights()
-        for u in range(1, OPENING_UNITS):
-            if u % CHUNK_UNITS == 0:
-                load(LOADS_AHEAD + u // CHUNK_UNITS - 1, [CHUNK_TILES])
-            advance(transpose_and_regroup, (u + 1) * UNIT_BANKS)
-            advance(quantise, u)
-            advance(project, u - 1)
-            advance(add_bias, u - 1)
-            advance(moments_of_pairs, u - 2)
-
-        for step in range(OPENING_UNITS // CHUNK_UNITS, N_CHUNKS):
-            if step + LOADS_AHEAD - 1 < N_CHUNKS:
+        for step in range(N_CHUNKS):
+            if 1 <= step <= N_CHUNKS - LOADS_AHEAD:
                 load(step + LOADS_AHEAD - 1, [CHUNK_TILES])
             c = step - LAG_NORMALISE
-            advance(quantise, step * CHUNK_UNITS - 1)
+            if step >= 1:
+                quantise(2 * step - 2)
+            if c >= 2:
+                shift_keys(c - 2, nc.vector, ALL)
+                store_keys(c - 2, ALL)
             if c >= 0:
-                row_factors(c)
-                row_offsets(c)
-            advance(quantise, step * CHUNK_UNITS)
+                row_factors(c, ALL)
+                row_offsets(c, ALL)
+            if step >= 1:
+                quantise(2 * step - 1)
             if c >= 1:
-                shift_keys(c - 1, nc.vector, ALL)
-                store_keys(c - 1)
-            advance(transpose_and_regroup, step * CHUNK_BANKS + 1)
-            if c >= 0:
-                normalise(c, ALL)
-            if c >= 1:
-                apply_gain(c, nc.gpsimd, scaled_pool)
-            advance(transpose_and_regroup, (step + 1) * CHUNK_BANKS)
-            advance(project, step * CHUNK_UNITS)
-            advance(add_bias, (step - 1) * CHUNK_UNITS)
-            advance(moments_of_pairs, (step - 1) * CHUNK_UNITS)
-            if c == 0:
-                apply_gain(c, nc.vector, scaled_pool)
+                apply_gain(c - 1, nc.gpsimd, scaled_pool, ALL)
+            for b in range(CHUNK_BANKS):
+                transpose_and_regroup(step * CHUNK_BANKS + b)
+                if step == 0 and b == 1:
+                    prepare_weights()
+                if c >= 0 and b == 0:
+                    normalise(c, ALL)
+            if step >= 1:
+                project(2 * step - 2)
+                project(2 * step - 1)
+            if step >= 2:
+                for stage in (add_bias, moments_of_pairs):
+                    stage(2 * step - 4)
+                    stage(2 * step - 3)
 
-        advance(quantise, N_UNITS)
-        row_factors(LAST - 2)
-        row_offsets(LAST - 2)
-        shift_keys(LAST - 3, nc.vector, ALL)
-        store_keys(LAST - 3)
+        a, b = 2 * LAST, 2 * LAST + 1
+        quantise(a)
+        shift_keys(LAST - 4, nc.vector, ALL)
+        store_keys(LAST - 4, ALL)
+        row_factors(LAST - 2, ALL)
+        row_offsets(LAST - 2, ALL)
+        quantise(b)
+        apply_gain(LAST - 3, nc.gpsimd, scaled_pool, ALL)
         normalise(LAST - 2, ALL)
-        apply_gain(LAST - 2, nc.gpsimd, out_pool)
-        advance(project, N_UNITS)
-        advance(add_bias, N_UNITS - CHUNK_UNITS)
-        advance(moments_of_pairs, N_UNITS - CHUNK_UNITS)
-        row_factors(LAST - 1)
-        advance(add_bias, N_UNITS - 1)
-        row_offsets(LAST - 1)
-        advance(add_bias, N_UNITS)
+        apply_gain(LAST - 2, nc.gpsimd, out_pool, ALL)
+        project(a)
+        project(b)
+        for stage in (add_bias, moments_of_pairs):
+            stage(a - 2)
+            stage(b - 2)
+        row_factors(LAST - 1, ALL)
+        add_bias(a)
+        add_bias(b)
+        shift_keys(LAST - 3, nc.vector, ALL)
+        store_keys(LAST - 3, ALL)
+        row_offsets(LAST - 1, ALL)
+        moments_of_pairs(a)
+
+        moments_of_pairs(b)
+
         normalise(LAST - 1, ALL)
-        advance(moments_of_pairs, N_UNITS)
-        row_factors(LAST)
+        row_factors(LAST, ALL)
         shift_keys(LAST - 2, nc.vector, ALL)
-        store_keys(LAST - 2)
-        row_offsets(LAST)
+        store_keys(LAST - 2, ALL)
+        row_offsets(LAST, ALL)
         normalise(LAST, ALL)
         for half in (FIRST, SECOND):
             apply_gain(LAST - 1, nc.vector, out_pool, half)
         for half in (FIRST, SECOND):
             shift_keys(LAST - 1, nc.vector, half)
-        store_keys(LAST - 1)
+        store_keys(LAST - 1, ALL)
         for half in (FIRST, SECOND):
             apply_gain(LAST, nc.vector, out_pool, half)
         for half in (FIRST, SECOND):

@@ -280,9 +280,8 @@ def tile_crossattention2d_rope_pb_t_kernel(tc, y, wkv, bkv, kn_g, kn_b, out_0, o
                     prepare_weights()
                 if c >= 0 and b == 0:
                     normalise(c, ALL)
-            if step >= 1:
-                project(2 * step - 2)
-                project(2 * step - 1)
+                if step >= 1 and b % UNIT_BANKS == UNIT_BANKS - 1:
+                    project(2 * step - 2 + b // UNIT_BANKS)
             if step >= 2:
                 for stage in (add_bias, moments_of_pairs):
                     stage(2 * step - 4)

@@ -10,7 +10,6 @@ U8 = mybir.dt.uint8
 FP8X4 = mybir.dt.float8_e4m3fn_x4
 ALU = mybir.AluOpType
 ACT = mybir.ActivationFunctionType
-AXIS = mybir.AxisListType
 
 P = 128
 K = 512
@@ -26,12 +25,20 @@ BANK_ROWS = BANK_TILES * P
 UNIT_BANKS = UNIT_TILES // BANK_TILES
 CHUNK_TILES = 8
 CHUNK_UNITS = CHUNK_TILES // UNIT_TILES
+CHUNK_BANKS = CHUNK_TILES // BANK_TILES
 N_CHUNKS = ROWS // (CHUNK_TILES * P)
+LAST = N_CHUNKS - 1
+
+ALL = slice(0, CHUNK_TILES)
+FIRST = slice(0, UNIT_TILES)
+SECOND = slice(UNIT_TILES, CHUNK_TILES)
+BY_VECTOR = slice(0, 6)
+BY_GPSIMD = slice(6, CHUNK_TILES)
 
 LAG_NORMALISE = 3
-N_UNITS = N_CHUNKS * CHUNK_UNITS
-OPENING_UNITS = 4
-CHUNK_BANKS = CHUNK_UNITS * UNIT_BANKS
+LAG_GAIN = 4
+LAG_SHIFT = 5
+LAG_BIAS_UNITS = 3
 
 LOADS_AHEAD = 6
 CHUNKS_IN_PIECES = 4
@@ -54,35 +61,34 @@ def tile_crossattention2d_rope_pb_t_kernel(tc, y, wkv, bkv, kn_g, kn_b, out_0, o
         codes_pool = ctx.enter_context(tc.tile_pool(name="codes_pool", bufs=4))
         x_pool = ctx.enter_context(tc.tile_pool(name="x_pool", bufs=6))
         stat_pool = ctx.enter_context(tc.tile_pool(name="stat_pool", bufs=6))
-        scaled_pool = ctx.enter_context(tc.tile_pool(name="scaled_pool", bufs=1))
         xhat_pool = ctx.enter_context(tc.tile_pool(name="xhat_pool", bufs=4))
+        scaled_pool = ctx.enter_context(tc.tile_pool(name="scaled_pool", bufs=2))
         out_pool = ctx.enter_context(tc.tile_pool(name="out_pool", bufs=4))
         words_psum = ctx.enter_context(tc.psum_pool(name="words_psum", bufs=4))
-        product_psum = ctx.enter_context(tc.psum_pool(name="product_psum", bufs=4))
+        product_psum = ctx.enter_context(tc.psum_pool(name="product_psum", bufs=3))
+        vector_psum = ctx.enter_context(tc.psum_pool(name="vector_psum", bufs=1))
 
         y_tiles = {}
 
-        def load(c, pieces):
-            start = 0
-            for i, tiles in enumerate(pieces):
-                piece = y_pool.tile([P, tiles * K], BF16, name="y_%d_%d" % (c, start))
-                nc.sync.dma_start(out=piece[:], in_=y_chunks[c][:, start * K : (start + tiles) * K])
+        def load(c, tiles):
+            for first in range(0, CHUNK_TILES, tiles):
+                piece = y_pool.tile([P, tiles * K], BF16, name="y_%d_%d" % (c, first))
+                nc.sync.dma_start(out=piece[:], in_=y_chunks[c][:, first * K : (first + tiles) * K])
                 for j in range(tiles):
-                    y_tiles[(c, start + j)] = piece[:, j * K : (j + 1) * K]
-                start += tiles
-                if c == 0 and i == 1:
+                    y_tiles[(c, first + j)] = piece[:, j * K : (j + 1) * K]
+                if c == 0 and first == BANK_TILES:
                     nc.sync.dma_start(out=w_rows[:], in_=wkv)
 
         w_rows = consts.tile([P, K], BF16, name="w_rows")
         vectors_bf16 = consts.tile([P, 2 * P], BF16, name="vectors_bf16")
         for c in range(CHUNKS_IN_PIECES):
-            load(c, [2,2,2,2] if c == 0 else [BANK_TILES] * (CHUNK_TILES // BANK_TILES))
+            load(c, BANK_TILES)
             if c == 0:
                 nc.sync.dma_start(out=vectors_bf16[:, 0:P], in_=bkv.partition_broadcast(P))
         nc.sync.dma_start(out=vectors_bf16[:, P : P + KEYS], in_=kn_g.partition_broadcast(P))
         nc.sync.dma_start(out=vectors_bf16[:, P + KEYS : 2 * P], in_=kn_b.partition_broadcast(P))
         for c in range(CHUNKS_IN_PIECES, LOADS_AHEAD):
-            load(c, [CHUNK_TILES])
+            load(c, CHUNK_TILES)
 
         eps = consts.tile([P, 1], F32, name="eps")
         nc.vector.memset(eps[:], EPS)
@@ -90,6 +96,7 @@ def tile_crossattention2d_rope_pb_t_kernel(tc, y, wkv, bkv, kn_g, kn_b, out_0, o
         nc.scalar.activation(out=table_warmer[:], in_=eps[:], func=ACT.Abs_reciprocal_sqrt)
         identity = consts.tile([P, P], F32, name="identity")
         make_identity(nc, identity[:])
+        identity_bf16 = consts.tile([P, P], BF16, name="identity_bf16")
 
         w_grouped = consts.tile([P, 4 * P], BF16, name="w_grouped", align_bytes=64)
         w_codes = consts.tile([P, P], U32, name="w_codes", align_bytes=64)
@@ -104,6 +111,7 @@ def tile_crossattention2d_rope_pb_t_kernel(tc, y, wkv, bkv, kn_g, kn_b, out_0, o
                 in_=w_words[:].rearrange("p h f -> p f h"),
             )
             nc.vector.quantize_mx(out=w_codes[:].bitcast(FP8X4), scales=w_scales[:], in_=w_grouped[:])
+            nc.vector.tensor_copy(out=identity_bf16[:], in_=identity[:])
 
         def repeated(vector, n):
             return vector.unsqueeze(1).to_broadcast([P, n] + list(vector.shape[1:]))
@@ -111,6 +119,13 @@ def tile_crossattention2d_rope_pb_t_kernel(tc, y, wkv, bkv, kn_g, kn_b, out_0, o
         bias = vectors_bf16[:, 0:P].rearrange("p (h f) -> p h f", h=2)
         gain = vectors_bf16[:, P : P + KEYS]
         shift = vectors_bf16[:, P + KEYS : 2 * P]
+
+        vector_bank = vector_psum.tile([P, 2 * KEYS], F32, name="vector_bank")
+        gain_psum = vector_bank[:, 0:KEYS]
+        shift_psum = vector_bank[:, KEYS : 2 * KEYS]
+
+        def copy_vectors_to_psum():
+            nc.tensor.matmul(vector_bank[:], lhsT=identity_bf16[:], rhs=vectors_bf16[:, P : 2 * P], start=True, stop=True)
 
         grouped = {}
         y_codes = {}
@@ -127,22 +142,19 @@ def tile_crossattention2d_rope_pb_t_kernel(tc, y, wkv, bkv, kn_g, kn_b, out_0, o
         def place(u):
             return u // CHUNK_UNITS, (u % CHUNK_UNITS) * UNIT_TILES
 
-        def units(c):
-            return range(c * CHUNK_UNITS, (c + 1) * CHUNK_UNITS)
-
         def transpose_and_regroup(b):
-            u, half = b // UNIT_BANKS, b % UNIT_BANKS
+            u, part = b // UNIT_BANKS, b % UNIT_BANKS
             c, first = place(u)
-            if half == 0:
+            if part == 0:
                 grouped[u] = grouped_pool.tile([P, 4 * UNIT_ROWS], BF16, name="grouped", align_bytes=64)
             pairs = grouped[u][:].bitcast(F32).rearrange("p (r h) -> p r h", h=2)
             bank = words_psum.tile([P, 2, BANK_ROWS], F32, tag="words", name="bank")
             for i in range(BANK_TILES):
-                words = y_tiles[(c, first + half * BANK_TILES + i)].bitcast(F32)
+                words = y_tiles[(c, first + part * BANK_TILES + i)].bitcast(F32)
                 for h in range(2):
                     nc.tensor.transpose(bank[:, h, i * P : (i + 1) * P], words[:, h : ROW_WORDS : 2], identity[:])
             nc.scalar.copy(
-                out=pairs[:, half * BANK_ROWS : (half + 1) * BANK_ROWS, :], in_=bank[:].rearrange("p h r -> p r h")
+                out=pairs[:, part * BANK_ROWS : (part + 1) * BANK_ROWS, :], in_=bank[:].rearrange("p h r -> p r h")
             )
 
         def quantise(u):
@@ -186,145 +198,152 @@ def tile_crossattention2d_rope_pb_t_kernel(tc, y, wkv, bkv, kn_g, kn_b, out_0, o
                     in_=x[c][:, 0, j : j + 2, :].rearrange("p j f -> p f j"),
                 )
 
-        def row_factors(c, tiles):
-            if c not in rstd:
-                rstd[c] = stat_pool.tile([P, CHUNK_TILES], F32, name="rstd")
+        def row_factors(c):
+            rstd[c] = stat_pool.tile([P, CHUNK_TILES], F32, name="rstd")
             nc.scalar.activation(
-                out=rstd[c][:, tiles],
-                in_=moments[c][:, tiles, 2],
+                out=rstd[c][:],
+                in_=moments[c][:, :, 2],
                 func=ACT.Abs_reciprocal_sqrt,
                 bias=eps[:, 0:1],
                 scale=1.0 / KEYS,
             )
 
-        def row_offsets(c, tiles):
-            if c not in offset:
-                offset[c] = stat_pool.tile([P, CHUNK_TILES], F32, name="offset")
+        def row_offsets(c):
+            offset[c] = stat_pool.tile([P, CHUNK_TILES], F32, name="offset")
             nc.vector.scalar_tensor_tensor(
-                out=offset[c][:, tiles],
-                in0=moments[c][:, tiles, 1],
-                scalar=-1.0,
-                in1=rstd[c][:, tiles],
-                op0=ALU.mult,
-                op1=ALU.mult,
+                out=offset[c][:], in0=moments[c][:, :, 1], scalar=-1.0, in1=rstd[c][:], op0=ALU.mult, op1=ALU.mult
             )
 
-        def normalise(c, tiles, on_scalar=True):
-            if c not in xhat:
-                xhat[c] = xhat_pool.tile([P, CHUNK_TILES, KEYS], F32, name="xhat")
-            for j in range(tiles.start, tiles.stop):
-                if on_scalar:
-                    nc.scalar.activation(
-                        out=xhat[c][:, j, :],
-                        in_=x[c][:, 0, j, :],
-                        func=ACT.Identity,
-                        bias=offset[c][:, j : j + 1],
-                        scale=rstd[c][:, j : j + 1],
-                    )
-                else:
-                    nc.vector.tensor_scalar(
-                        out=xhat[c][:, j, :],
-                        in0=x[c][:, 0, j, :],
-                        scalar1=rstd[c][:, j : j + 1],
-                        scalar2=offset[c][:, j : j + 1],
-                        op0=ALU.mult,
-                        op1=ALU.add,
-                    )
+        def normalise(c):
+            xhat[c] = xhat_pool.tile([P, CHUNK_TILES, KEYS], F32, name="xhat")
+            for j in range(CHUNK_TILES):
+                nc.scalar.activation(
+                    out=xhat[c][:, j, :],
+                    in_=x[c][:, 0, j, :],
+                    func=ACT.Identity,
+                    bias=offset[c][:, j : j + 1],
+                    scale=rstd[c][:, j : j + 1],
+                )
 
-        def apply_gain(c, engine, pool, tiles=slice(0, CHUNK_TILES)):
-            n = tiles.stop - tiles.start
-            if c not in scaled:
-                scaled[c] = pool.tile([P, CHUNK_TILES, KEYS], F32, name="scaled")
-            engine.tensor_tensor(out=scaled[c][:, tiles, :], in0=xhat[c][:, tiles, :], in1=repeated(gain, n), op=ALU.mult)
+        def open_scaled(c):
+            scaled[c] = scaled_pool.tile([P, CHUNK_TILES, KEYS], F32, name="scaled")
+            nc.vector.memset(scaled[c][:, 0, 0:2], 0.0)
 
-        def shift_keys(c, engine, tiles):
-            n = tiles.stop - tiles.start
+        def gain_by_gpsimd(c):
+            nc.gpsimd.tensor_tensor(out=scaled[c][:], in0=xhat[c][:], in1=repeated(gain, CHUNK_TILES), op=ALU.mult)
+
+        def gain_by_vector(c, tiles):
+            nc.vector.tensor_tensor(
+                out=scaled[c][:, tiles, :],
+                in0=xhat[c][:, tiles, :],
+                in1=repeated(gain_psum, tiles.stop - tiles.start),
+                op=ALU.mult,
+            )
+
+        def apply_shift(engine, vector, c, tiles):
             if c not in keys:
                 keys[c] = out_pool.tile([P, CHUNK_TILES, KEYS], F32, name="keys")
-            engine.tensor_tensor(out=keys[c][:, tiles, :], in0=scaled[c][:, tiles, :], in1=repeated(shift, n), op=ALU.add)
+            engine.tensor_tensor(
+                out=keys[c][:, tiles, :],
+                in0=scaled[c][:, tiles, :],
+                in1=repeated(vector, tiles.stop - tiles.start),
+                op=ALU.add,
+            )
 
-        def store_keys(c, tiles=slice(0, CHUNK_TILES)):
+        def shift_by_gpsimd(c, tiles):
+            apply_shift(nc.gpsimd, shift, c, tiles)
+
+        def shift_by_vector(c, tiles):
+            apply_shift(nc.vector, shift_psum, c, tiles)
+
+        def store_keys(c, tiles):
             nc.sync.dma_start(
                 out=key_chunks[c][:, tiles.start * KEYS : tiles.stop * KEYS],
                 in_=keys[c][:, tiles, :].rearrange("p j f -> p (j f)"),
             )
 
-        def shift_and_store(c, engine, tiles=slice(0, CHUNK_TILES)):
-            shift_keys(c, engine, tiles)
-            store_keys(c, tiles)
-
-        ALL = slice(0, CHUNK_TILES)
-        FIRST = slice(0, UNIT_TILES)
-        SECOND = slice(UNIT_TILES, CHUNK_TILES)
-        LAST = N_CHUNKS - 1
+        def chunk_at(step, lag):
+            return step - lag if step >= lag else None
 
         for step in range(N_CHUNKS):
             if 1 <= step <= N_CHUNKS - LOADS_AHEAD:
-                load(step + LOADS_AHEAD - 1, [CHUNK_TILES])
-            c = step - LAG_NORMALISE
+                load(step + LOADS_AHEAD - 1, CHUNK_TILES)
+            normalised = chunk_at(step, LAG_NORMALISE)
+            gained = chunk_at(step, LAG_GAIN)
+            shifted = chunk_at(step, LAG_SHIFT)
+            first_unit = step * CHUNK_UNITS
+
             if step >= 1:
-                quantise(2 * step - 2)
-            if c >= 2:
-                shift_keys(c - 2, nc.vector, ALL)
-                store_keys(c - 2, ALL)
-            if c >= 0:
-                row_factors(c, ALL)
-                row_offsets(c, ALL)
+                quantise(first_unit - 2)
+            if normalised is not None:
+                row_factors(normalised)
+                row_offsets(normalised)
+            if gained is not None:
+                open_scaled(gained)
             if step >= 1:
-                quantise(2 * step - 1)
-            if c >= 1:
-                apply_gain(c - 1, nc.gpsimd, scaled_pool, ALL)
+                quantise(first_unit - 1)
+            if gained is not None:
+                gain_by_gpsimd(gained)
+                shift_by_gpsimd(gained, BY_GPSIMD)
+            if shifted is not None:
+                shift_by_vector(shifted, BY_VECTOR)
+                store_keys(shifted, ALL)
+
             for b in range(CHUNK_BANKS):
                 transpose_and_regroup(step * CHUNK_BANKS + b)
                 if step == 0 and b == 1:
                     prepare_weights()
-                if c >= 0 and b == 0:
-                    normalise(c, ALL)
+                if step == LAG_GAIN and b == CHUNK_BANKS - 1:
+                    copy_vectors_to_psum()
+                if normalised is not None and b == 0:
+                    normalise(normalised)
                 if step >= 1 and b % UNIT_BANKS == UNIT_BANKS - 1:
-                    project(2 * step - 2 + b // UNIT_BANKS)
-            if step >= 2:
-                for stage in (add_bias, moments_of_pairs):
-                    stage(2 * step - 4)
-                    stage(2 * step - 3)
+                    project(first_unit - 2 + b // UNIT_BANKS)
 
-        a, b = 2 * LAST, 2 * LAST + 1
+            units = [u for u in (first_unit - LAG_BIAS_UNITS, first_unit - LAG_BIAS_UNITS + 1) if u >= 0]
+            for u in units:
+                add_bias(u)
+            for u in units:
+                moments_of_pairs(u)
+
+        a, b = LAST * CHUNK_UNITS, LAST * CHUNK_UNITS + 1
         quantise(a)
-        shift_keys(LAST - 4, nc.vector, ALL)
-        store_keys(LAST - 4, ALL)
-        row_factors(LAST - 2, ALL)
-        row_offsets(LAST - 2, ALL)
+        row_factors(LAST - 2)
+        row_offsets(LAST - 2)
+        open_scaled(LAST - 3)
         quantise(b)
-        apply_gain(LAST - 3, nc.gpsimd, scaled_pool, ALL)
-        normalise(LAST - 2, ALL)
-        apply_gain(LAST - 2, nc.gpsimd, out_pool, ALL)
+        gain_by_gpsimd(LAST - 3)
+        shift_by_vector(LAST - 4, BY_VECTOR)
+        store_keys(LAST - 4, ALL)
+        normalise(LAST - 2)
+        for c in (LAST - 2, LAST - 1, LAST):
+            scaled[c] = out_pool.tile([P, CHUNK_TILES, KEYS], F32, name="scaled")
+        gain_by_gpsimd(LAST - 2)
         project(a)
         project(b)
-        for stage in (add_bias, moments_of_pairs):
-            stage(a - 2)
-            stage(b - 2)
-        row_factors(LAST - 1, ALL)
+        add_bias(b - 2)
         add_bias(a)
+        moments_of_pairs(b - 2)
+        row_factors(LAST - 1)
         add_bias(b)
-        shift_keys(LAST - 3, nc.vector, ALL)
-        store_keys(LAST - 3, ALL)
-        row_offsets(LAST - 1, ALL)
         moments_of_pairs(a)
-
         moments_of_pairs(b)
-
-        normalise(LAST - 1, ALL)
-        row_factors(LAST, ALL)
-        shift_keys(LAST - 2, nc.vector, ALL)
+        row_offsets(LAST - 1)
+        normalise(LAST - 1)
+        row_factors(LAST)
+        shift_by_vector(LAST - 3, ALL)
+        store_keys(LAST - 3, ALL)
+        shift_by_vector(LAST - 2, ALL)
         store_keys(LAST - 2, ALL)
-        row_offsets(LAST, ALL)
-        normalise(LAST, ALL)
-        for half in (FIRST, SECOND):
-            apply_gain(LAST - 1, nc.vector, out_pool, half)
-        for half in (FIRST, SECOND):
-            shift_keys(LAST - 1, nc.vector, half)
+        row_offsets(LAST)
+        normalise(LAST)
+        for tiles in (FIRST, SECOND):
+            gain_by_vector(LAST - 1, tiles)
+        for tiles in (FIRST, SECOND):
+            shift_by_vector(LAST - 1, tiles)
         store_keys(LAST - 1, ALL)
-        for half in (FIRST, SECOND):
-            apply_gain(LAST, nc.vector, out_pool, half)
-        for half in (FIRST, SECOND):
-            shift_keys(LAST, nc.vector, half)
-            store_keys(LAST, half)
+        for tiles in (FIRST, SECOND):
+            gain_by_vector(LAST, tiles)
+        for tiles in (FIRST, SECOND):
+            shift_by_vector(LAST, tiles)
+            store_keys(LAST, tiles)

from contextlib import ExitStack

import concourse.mybir as mybir
from concourse.masks import make_identity

F32 = mybir.dt.float32
BF16 = mybir.dt.bfloat16
U32 = mybir.dt.uint32
U8 = mybir.dt.uint8
FP8X4 = mybir.dt.float8_e4m3fn_x4
ALU = mybir.AluOpType
ACT = mybir.ActivationFunctionType

P = 128
K = 512
ROW_WORDS = K // 2
KEYS = 64
ROWS = 8 * 2048
EPS = 1e-6

UNIT_TILES = 4
UNIT_ROWS = UNIT_TILES * P
BANK_TILES = 2
BANK_ROWS = BANK_TILES * P
UNIT_BANKS = UNIT_TILES // BANK_TILES
CHUNK_TILES = 8
CHUNK_UNITS = CHUNK_TILES // UNIT_TILES
CHUNK_BANKS = CHUNK_TILES // BANK_TILES
N_CHUNKS = ROWS // (CHUNK_TILES * P)
LAST = N_CHUNKS - 1

ALL = slice(0, CHUNK_TILES)
FIRST = slice(0, UNIT_TILES)
SECOND = slice(UNIT_TILES, CHUNK_TILES)
BY_VECTOR = slice(0, 6)
BY_GPSIMD = slice(6, CHUNK_TILES)

LAG_NORMALISE = 3
LAG_GAIN = 4
LAG_SHIFT = 5
LAG_BIAS_UNITS = 3

LOADS_AHEAD = 6
CHUNKS_IN_PIECES = 4

FLOPS = 2 * ROWS * K * P


def tile_crossattention2d_rope_pb_t_kernel(tc, y, wkv, bkv, kn_g, kn_b, out_0, out_1):
    nc = tc.nc

    y_chunks = y.flatten_outer_dims().rearrange("(c p j) k -> c p (j k)", p=P, j=CHUNK_TILES)
    key_chunks = out_0.flatten_outer_dims().rearrange("(c p j) f -> c p (j f)", p=P, j=CHUNK_TILES)
    value_chunks = out_1.flatten_outer_dims().rearrange("(c p j) f -> c p (j f)", p=P, j=CHUNK_TILES)

    with ExitStack() as ctx:
        ctx.enter_context(tc.manual_schedule())
        consts = ctx.enter_context(tc.tile_pool(name="consts", bufs=1))
        y_pool = ctx.enter_context(tc.tile_pool(name="y_pool", bufs=1))
        grouped_pool = ctx.enter_context(tc.tile_pool(name="grouped_pool", bufs=4))
        codes_pool = ctx.enter_context(tc.tile_pool(name="codes_pool", bufs=4))
        x_pool = ctx.enter_context(tc.tile_pool(name="x_pool", bufs=6))
        stat_pool = ctx.enter_context(tc.tile_pool(name="stat_pool", bufs=6))
        xhat_pool = ctx.enter_context(tc.tile_pool(name="xhat_pool", bufs=4))
        scaled_pool = ctx.enter_context(tc.tile_pool(name="scaled_pool", bufs=2))
        out_pool = ctx.enter_context(tc.tile_pool(name="out_pool", bufs=4))
        words_psum = ctx.enter_context(tc.psum_pool(name="words_psum", bufs=4))
        product_psum = ctx.enter_context(tc.psum_pool(name="product_psum", bufs=3))
        vector_psum = ctx.enter_context(tc.psum_pool(name="vector_psum", bufs=1))

        y_tiles = {}

        def load(c, tiles):
            for first in range(0, CHUNK_TILES, tiles):
                piece = y_pool.tile([P, tiles * K], BF16, name="y_%d_%d" % (c, first))
                nc.sync.dma_start(out=piece[:], in_=y_chunks[c][:, first * K : (first + tiles) * K])
                for j in range(tiles):
                    y_tiles[(c, first + j)] = piece[:, j * K : (j + 1) * K]
                if c == 0 and first == BANK_TILES:
                    nc.sync.dma_start(out=w_rows[:], in_=wkv)

        w_rows = consts.tile([P, K], BF16, name="w_rows")
        vectors_bf16 = consts.tile([P, 2 * P], BF16, name="vectors_bf16")
        for c in range(CHUNKS_IN_PIECES):
            load(c, BANK_TILES)
            if c == 0:
                nc.sync.dma_start(out=vectors_bf16[:, 0:P], in_=bkv.partition_broadcast(P))
        nc.sync.dma_start(out=vectors_bf16[:, P : P + KEYS], in_=kn_g.partition_broadcast(P))
        nc.sync.dma_start(out=vectors_bf16[:, P + KEYS : 2 * P], in_=kn_b.partition_broadcast(P))
        for c in range(CHUNKS_IN_PIECES, LOADS_AHEAD):
            load(c, CHUNK_TILES)

        eps = consts.tile([P, 1], F32, name="eps")
        nc.vector.memset(eps[:], EPS)
        table_warmer = consts.tile([P, 1], F32, name="table_warmer")
        nc.scalar.activation(out=table_warmer[:], in_=eps[:], func=ACT.Abs_reciprocal_sqrt)
        identity = consts.tile([P, P], F32, name="identity")
        make_identity(nc, identity[:])
        identity_bf16 = consts.tile([P, P], BF16, name="identity_bf16")

        w_grouped = consts.tile([P, 4 * P], BF16, name="w_grouped", align_bytes=64)
        w_codes = consts.tile([P, P], U32, name="w_codes", align_bytes=64)
        w_scales = consts.tile([P, P], U8, name="w_scales", align_bytes=64)

        def prepare_weights():
            w_words = words_psum.tile([P, 2, P], F32, tag="words", name="w_words")
            for h in range(2):
                nc.tensor.transpose(w_words[:, h, :], w_rows[:].bitcast(F32)[:, h : ROW_WORDS : 2], identity[:])
            nc.vector.tensor_copy(
                out=w_grouped[:].bitcast(F32).rearrange("p (f h) -> p f h", h=2),
                in_=w_words[:].rearrange("p h f -> p f h"),
            )
            nc.vector.quantize_mx(out=w_codes[:].bitcast(FP8X4), scales=w_scales[:], in_=w_grouped[:])
            nc.vector.tensor_copy(out=identity_bf16[:], in_=identity[:])

        def repeated(vector, n):
            return vector.unsqueeze(1).to_broadcast([P, n] + list(vector.shape[1:]))

        bias = vectors_bf16[:, 0:P].rearrange("p (h f) -> p h f", h=2)
        gain = vectors_bf16[:, P : P + KEYS]
        shift = vectors_bf16[:, P + KEYS : 2 * P]

        vector_bank = vector_psum.tile([P, 2 * KEYS], F32, name="vector_bank")
        gain_psum = vector_bank[:, 0:KEYS]
        shift_psum = vector_bank[:, KEYS : 2 * KEYS]

        def copy_vectors_to_psum():
            nc.tensor.matmul(vector_bank[:], lhsT=identity_bf16[:], rhs=vectors_bf16[:, P : 2 * P], start=True, stop=True)

        grouped = {}
        y_codes = {}
        y_scales = {}
        product = {}
        x = {}
        moments = {}
        rstd = {}
        offset = {}
        xhat = {}
        scaled = {}
        keys = {}

        def place(u):
            return u // CHUNK_UNITS, (u % CHUNK_UNITS) * UNIT_TILES

        def transpose_and_regroup(b):
            u, part = b // UNIT_BANKS, b % UNIT_BANKS
            c, first = place(u)
            if part == 0:
                grouped[u] = grouped_pool.tile([P, 4 * UNIT_ROWS], BF16, name="grouped", align_bytes=64)
            pairs = grouped[u][:].bitcast(F32).rearrange("p (r h) -> p r h", h=2)
            bank = words_psum.tile([P, 2, BANK_ROWS], F32, tag="words", name="bank")
            for i in range(BANK_TILES):
                words = y_tiles[(c, first + part * BANK_TILES + i)].bitcast(F32)
                for h in range(2):
                    nc.tensor.transpose(bank[:, h, i * P : (i + 1) * P], words[:, h : ROW_WORDS : 2], identity[:])
            nc.scalar.copy(
                out=pairs[:, part * BANK_ROWS : (part + 1) * BANK_ROWS, :], in_=bank[:].rearrange("p h r -> p r h")
            )

        def quantise(u):
            y_codes[u] = codes_pool.tile([P, UNIT_ROWS], U32, name="y_codes", align_bytes=64)
            y_scales[u] = codes_pool.tile([P, UNIT_ROWS], U8, name="y_scales", align_bytes=64)
            nc.vector.quantize_mx(out=y_codes[u][:].bitcast(FP8X4), scales=y_scales[u][:], in_=grouped[u][:])

        def project(u):
            product[u] = product_psum.tile([P, UNIT_TILES, P], F32, name="product")
            for i in range(UNIT_TILES):
                nc.tensor.matmul_mx(
                    out=product[u][:, i, :],
                    lhsT=y_codes[u][:, i * P : (i + 1) * P].bitcast(FP8X4),
                    lhsT_scale=y_scales[u][:, i * P : (i + 1) * P],
                    rhs=w_codes[:].bitcast(FP8X4),
                    rhs_scale=w_scales[:],
                    start=True,
                    stop=True,
                )

        def add_bias(u):
            c, first = place(u)
            if first == 0:
                x[c] = x_pool.tile([P, 2, CHUNK_TILES, KEYS], F32, name="x")
            nc.vector.tensor_tensor(
                out=x[c][:, :, first : first + UNIT_TILES, :].rearrange("p h j f -> p j h f"),
                in0=product[u][:].rearrange("p j (h f) -> p j h f", h=2),
                in1=repeated(bias, UNIT_TILES),
                op=ALU.add,
            )
            if first + UNIT_TILES == CHUNK_TILES:
                nc.sync.dma_start(out=value_chunks[c], in_=x[c][:, 1, :, :].rearrange("p j f -> p (j f)"))

        def moments_of_pairs(u):
            c, first = place(u)
            if first == 0:
                moments[c] = stat_pool.tile([P, CHUNK_TILES, 3], F32, name="moments")
            for j in range(first, first + UNIT_TILES, 2):
                nc.vector.bn_stats(
                    out=moments[c][:, j : j + 2, :].rearrange("p j m -> p (j m)"),
                    in_=x[c][:, 0, j : j + 2, :].rearrange("p j f -> p f j"),
                )

        def row_factors(c):
            rstd[c] = stat_pool.tile([P, CHUNK_TILES], F32, name="rstd")
            nc.scalar.activation(
                out=rstd[c][:],
                in_=moments[c][:, :, 2],
                func=ACT.Abs_reciprocal_sqrt,
                bias=eps[:, 0:1],
                scale=1.0 / KEYS,
            )

        def row_offsets(c):
            offset[c] = stat_pool.tile([P, CHUNK_TILES], F32, name="offset")
            nc.vector.scalar_tensor_tensor(
                out=offset[c][:], in0=moments[c][:, :, 1], scalar=-1.0, in1=rstd[c][:], op0=ALU.mult, op1=ALU.mult
            )

        def normalise(c):
            xhat[c] = xhat_pool.tile([P, CHUNK_TILES, KEYS], F32, name="xhat")
            for j in range(CHUNK_TILES):
                nc.scalar.activation(
                    out=xhat[c][:, j, :],
                    in_=x[c][:, 0, j, :],
                    func=ACT.Identity,
                    bias=offset[c][:, j : j + 1],
                    scale=rstd[c][:, j : j + 1],
                )

        def open_scaled(c):
            scaled[c] = scaled_pool.tile([P, CHUNK_TILES, KEYS], F32, name="scaled")
            nc.vector.memset(scaled[c][:, 0, 0:2], 0.0)

        def gain_by_gpsimd(c):
            nc.gpsimd.tensor_tensor(out=scaled[c][:], in0=xhat[c][:], in1=repeated(gain, CHUNK_TILES), op=ALU.mult)

        def gain_by_vector(c, tiles):
            nc.vector.tensor_tensor(
                out=scaled[c][:, tiles, :],
                in0=xhat[c][:, tiles, :],
                in1=repeated(gain_psum, tiles.stop - tiles.start),
                op=ALU.mult,
            )

        def apply_shift(engine, vector, c, tiles):
            if c not in keys:
                keys[c] = out_pool.tile([P, CHUNK_TILES, KEYS], F32, name="keys")
            engine.tensor_tensor(
                out=keys[c][:, tiles, :],
                in0=scaled[c][:, tiles, :],
                in1=repeated(vector, tiles.stop - tiles.start),
                op=ALU.add,
            )

        def shift_by_gpsimd(c, tiles):
            apply_shift(nc.gpsimd, shift, c, tiles)

        def shift_by_vector(c, tiles):
            apply_shift(nc.vector, shift_psum, c, tiles)

        def store_keys(c, tiles):
            nc.sync.dma_start(
                out=key_chunks[c][:, tiles.start * KEYS : tiles.stop * KEYS],
                in_=keys[c][:, tiles, :].rearrange("p j f -> p (j f)"),
            )

        def chunk_at(step, lag):
            return step - lag if step >= lag else None

        for step in range(N_CHUNKS):
            if 1 <= step <= N_CHUNKS - LOADS_AHEAD:
                load(step + LOADS_AHEAD - 1, CHUNK_TILES)
            normalised = chunk_at(step, LAG_NORMALISE)
            gained = chunk_at(step, LAG_GAIN)
            shifted = chunk_at(step, LAG_SHIFT)
            first_unit = step * CHUNK_UNITS

            if step >= 1:
                quantise(first_unit - 2)
            if normalised is not None:
                row_factors(normalised)
                row_offsets(normalised)
            if gained is not None:
                open_scaled(gained)
            if step >= 1:
                quantise(first_unit - 1)
            if gained is not None:
                gain_by_gpsimd(gained)
                shift_by_gpsimd(gained, BY_GPSIMD)
            if shifted is not None:
                shift_by_vector(shifted, BY_VECTOR)
                store_keys(shifted, ALL)

            for b in range(CHUNK_BANKS):
                transpose_and_regroup(step * CHUNK_BANKS + b)
                if step == 0 and b == 1:
                    prepare_weights()
                if step == LAG_GAIN and b == CHUNK_BANKS - 1:
                    copy_vectors_to_psum()
                if normalised is not None and b == 0:
                    normalise(normalised)
                if step >= 1 and b % UNIT_BANKS == UNIT_BANKS - 1:
                    project(first_unit - 2 + b // UNIT_BANKS)

            units = [u for u in (first_unit - LAG_BIAS_UNITS, first_unit - LAG_BIAS_UNITS + 1) if u >= 0]
            for u in units:
                add_bias(u)
            for u in units:
                moments_of_pairs(u)

        a, b = LAST * CHUNK_UNITS, LAST * CHUNK_UNITS + 1
        quantise(a)
        row_factors(LAST - 2)
        row_offsets(LAST - 2)
        open_scaled(LAST - 3)
        quantise(b)
        gain_by_gpsimd(LAST - 3)
        shift_by_vector(LAST - 4, BY_VECTOR)
        store_keys(LAST - 4, ALL)
        normalise(LAST - 2)
        for c in (LAST - 2, LAST - 1, LAST):
            scaled[c] = out_pool.tile([P, CHUNK_TILES, KEYS], F32, name="scaled")
        gain_by_gpsimd(LAST - 2)
        project(a)
        project(b)
        add_bias(b - 2)
        add_bias(a)
        moments_of_pairs(b - 2)
        row_factors(LAST - 1)
        add_bias(b)
        moments_of_pairs(a)
        moments_of_pairs(b)
        row_offsets(LAST - 1)
        normalise(LAST - 1)
        row_factors(LAST)
        shift_by_vector(LAST - 3, ALL)
        store_keys(LAST - 3, ALL)
        shift_by_vector(LAST - 2, ALL)
        store_keys(LAST - 2, ALL)
        row_offsets(LAST)
        normalise(LAST)
        for tiles in (FIRST, SECOND):
            gain_by_vector(LAST - 1, tiles)
        for tiles in (FIRST, SECOND):
            shift_by_vector(LAST - 1, tiles)
        store_keys(LAST - 1, ALL)
        for tiles in (FIRST, SECOND):
            gain_by_vector(LAST, tiles)
        for tiles in (FIRST, SECOND):
            shift_by_vector(LAST, tiles)
            store_keys(LAST, tiles)
